import numpy as np
import ml_dtypes


def mxq(x, axis, fmt="e4m3"):
    dtype, down = {"e4m3": (ml_dtypes.float8_e4m3fn, 7), "e5m2": (ml_dtypes.float8_e5m2, 14)}[fmt]
    v = np.moveaxis(np.asarray(x, np.float32).astype(ml_dtypes.bfloat16).astype(np.float64), axis, -1)
    blocks = v.reshape(v.shape[:-1] + (-1, 32))
    amax = np.abs(blocks).max(-1, keepdims=True)
    byte = np.maximum(np.where(amax > 0, np.frexp(amax)[1] - 1 + 127, 0) - down, 1)
    scale = np.exp2(byte - 127.0)
    codes = (blocks / scale).astype(np.float32).astype(dtype).astype(np.float64)
    return np.moveaxis((codes * scale).reshape(v.shape), -1, axis)


WIDE = False


def mx_kscale(k):
    if not WIDE:
        return np.ones(k)
    levels = np.array([10, -10, 5, -5, 0])
    a = np.random.permutation(np.resize(levels, k // 512 * 4)).reshape(k // 512, 4)
    idx = np.arange(k)
    return np.exp2(a[idx // 512, idx % 128 // 32])


BF16 = ml_dtypes.bfloat16


def bf(x):
    return np.asarray(x, np.float32).astype(BF16)


def f64(x):
    return np.asarray(x).astype(np.float64)


B, N_VAR, D = 4096, 1, 512
NUM_UNITS = N_VAR * D


def sigmoid(v):
    return 1.0 / (1.0 + np.exp(-v))


def setup_inputs():
    s = mx_kscale(D)
    return {
        "inputs": bf(np.random.standard_normal((B, N_VAR))),
        "hidden": bf((np.random.standard_normal((B, D, N_VAR)) * s[None, :, None]).reshape(B, NUM_UNITS)),
        "gate_w_I2H": bf(np.random.standard_normal((N_VAR, 1, 2 * D, 1)) * 0.5),
        "gate_w_H2H": bf(np.random.standard_normal((N_VAR, 1, 2 * D, D)) / np.sqrt(D) / s),
        "gate_bias": bf(np.random.standard_normal(2 * NUM_UNITS) * 0.4),
        "update_w_I2H": bf(np.random.standard_normal((N_VAR, 1, D, 1)) * 0.5),
        "update_w_H2H": bf(np.random.standard_normal((N_VAR, 1, D, D)) * 1.5 / np.sqrt(D) / s),
        "update_bias": bf(np.random.standard_normal(NUM_UNITS) * 0.4),
    }


def reference(inputs, hidden, gate_w_I2H, gate_w_H2H, gate_bias, update_w_I2H, update_w_H2H, update_bias):
    inputs, hidden = f64(inputs), f64(hidden)
    b, num_units = hidden.shape
    n_var = inputs.shape[1]
    d = num_units // n_var

    x_v = inputs.T
    h_v = hidden.reshape(b, d, n_var).transpose(2, 0, 1)

    gx = x_v[:, :, None] * f64(gate_w_I2H)[:, 0, :, 0][:, None, :]
    gh = mxq(h_v, 2, "e4m3") @ mxq(f64(gate_w_H2H)[:, 0], 2, "e4m3").transpose(0, 2, 1)
    res_gate = (gx + gh).transpose(1, 0, 2).reshape(b, 2 * num_units) + f64(gate_bias)
    z, r = res_gate[:, :num_units], res_gate[:, num_units:]

    r_v = sigmoid(r).reshape(b, d, n_var).transpose(2, 0, 1)

    ux = x_v[:, :, None] * f64(update_w_I2H)[:, 0, :, 0][:, None, :]
    uh = mxq(h_v * r_v, 2, "e4m3") @ mxq(f64(update_w_H2H)[:, 0], 2, "e4m3").transpose(0, 2, 1)
    g = (ux + uh).transpose(1, 0, 2).reshape(b, num_units) + f64(update_bias)

    zs = sigmoid(z)
    return zs * hidden + (1.0 - zs) * np.tanh(g)

@@ -1,0 +1,334 @@
+from contextlib import ExitStack
+
+import concourse.mybir as mybir
+from concourse.masks import make_identity
+
+F32 = mybir.dt.float32
+BF16 = mybir.dt.bfloat16
+U32 = mybir.dt.uint32
+U8 = mybir.dt.uint8
+FP8X4 = mybir.dt.float8_e4m3fn_x4
+ALU = mybir.AluOpType
+ACT = mybir.ActivationFunctionType
+
+P = 128
+B = 4096
+D = 512
+FLOPS = 2 * B * D * 3 * D
+
+Z_PLANE = 0
+R_PLANE = 1
+G_PLANE = 2
+PINNED = True
+SIZES = [256, 512, 512, 512, 512, 512, 512, 512, 128, 128]
+V_TAIL = 2
+X_FIRST = SIZES[0] + SIZES[1]
+assert sum(SIZES) == B
+
+
+def tile_grucell_t_kernel(
+    tc, inputs, hidden, gate_w_I2H, gate_w_H2H, gate_bias, update_w_I2H, update_w_H2H, update_bias, out
+):
+    nc = tc.nc
+    nblk = len(SIZES)
+    starts = [sum(SIZES[:j]) for j in range(nblk)]
+    with ExitStack() as ctx:
+        const = ctx.enter_context(tc.tile_pool(name="const", bufs=1))
+        hpool = ctx.enter_context(tc.tile_pool(name="hpool", bufs=nblk))
+        p2 = ctx.enter_context(tc.tile_pool(name="p2", bufs=2))
+        p3 = ctx.enter_context(tc.tile_pool(name="p3", bufs=3))
+        p4 = ctx.enter_context(tc.tile_pool(name="p4", bufs=4))
+        tp = ctx.enter_context(tc.psum_pool(name="tp", bufs=2))
+        mxp = ctx.enter_context(tc.psum_pool(name="mxp", bufs=4))
+        flp = ctx.enter_context(tc.psum_pool(name="flp", bufs=2))
+        if PINNED:
+            ctx.enter_context(tc.manual_schedule())
+
+        ident = const.tile([P, P], F32, name="ident")
+        make_identity(nc, ident[:])
+        warm = const.tile([P, 1], F32, name="warm")
+        nc.vector.memset(warm[:], 0.0)
+        nc.scalar.activation(out=warm[:], in_=warm[:], func=ACT.Sigmoid)
+        prn = const.tile([P, 256], BF16, name="prn")
+        nc.vector.memset(prn[:], 0.0)
+
+        wn = {}
+        hn = {}
+
+        def load_w(plane, rows):
+            wnat = const.tile([P, 2048], BF16, name="wn%d" % plane)
+            nc.sync.dma_start(
+                out=wnat[:].rearrange("m (u x) -> m u x", u=2),
+                in_=rows.rearrange("a b (u m e) k -> m (a b u) (e k)", u=2, e=2),
+            )
+            wn[plane] = wnat
+
+        def load_h(queue, j):
+            size = SIZES[j]
+            hnat = hpool.tile([P, 2048], BF16, name="hn", tag="hn")
+            queue.dma_start(
+                out=hnat[:, 0 : 4 * size],
+                in_=hidden[starts[j] : starts[j] + size, :].rearrange("(p s) j -> p (s j)", s=size // P),
+            )
+            hn[j] = hnat
+
+        xb = const.tile([P, B], BF16, name="xb")
+        xrow = inputs.rearrange("b o -> (b o)")
+        load_w(R_PLANE, gate_w_H2H[:, :, D : 2 * D, :])
+        load_h(nc.scalar, 0)
+        nc.scalar.dma_start(out=prn[0:4, :], in_=gate_w_I2H.rearrange("a b (r k) c -> (a b r) (k c)", k=256))
+        nc.scalar.dma_start(out=prn[4:8, :], in_=gate_bias.rearrange("(r k) -> r k", k=256))
+        nc.scalar.dma_start(out=prn[8:10, :], in_=update_w_I2H.rearrange("a b (r k) c -> (a b r) (k c)", k=256))
+        nc.scalar.dma_start(out=prn[10:12, :], in_=update_bias.rearrange("(r k) -> r k", k=256))
+        nc.scalar.dma_start(out=xb[:, 0:X_FIRST], in_=xrow[0:X_FIRST].partition_broadcast(P))
+        load_w(Z_PLANE, gate_w_H2H[:, :, 0:D, :])
+        load_h(nc.sync, 1)
+        load_w(G_PLANE, update_w_H2H)
+        load_h(nc.sync, 2)
+        nc.sync.dma_start(out=xb[:, X_FIRST:B], in_=xrow[X_FIRST:B].partition_broadcast(P))
+        for j in range(3, nblk):
+            load_h(nc.sync, j)
+
+        wc = const.tile([P, 3 * 512], U32, name="wc", align_bytes=64)
+        ws = const.tile([P, 3 * 512], U8, name="ws", align_bytes=64)
+        gws = {}
+
+        def prep_w_tr(plane, engines):
+            words = wn[plane][:].bitcast(F32)
+            gw = const.tile([P, 2048], BF16, name="gw%d" % plane, align_bytes=64)
+            gww = gw[:].bitcast(F32)
+            for u in range(2):
+                bank = tp.tile([P, 512], F32, name="tpw", tag="tp")
+                for e in range(2):
+                    for kh in range(2):
+                        nc.tensor.transpose(
+                            out=bank[:, e * 256 + kh * 128 : e * 256 + kh * 128 + 128],
+                            in_=words[:, (2 * u + e) * 256 + kh * 128 : (2 * u + e) * 256 + kh * 128 + 128],
+                            identity=ident[:],
+                        )
+                dst = gww[:, u * 512 : (u + 1) * 512].rearrange("p (e m k) -> p e m k", e=2, k=2)
+                src = bank[:].rearrange("p (e k m) -> p e m k", e=2, k=2)
+                if engines[u] == "v":
+                    nc.vector.tensor_copy(out=dst, in_=src)
+                else:
+                    nc.scalar.copy(out=dst, in_=src)
+            gws[plane] = gw
+
+        def prep_w_q(plane):
+            nc.vector.quantize_mx(
+                out=wc[:, plane * 512 : (plane + 1) * 512].bitcast(FP8X4),
+                scales=ws[:, plane * 512 : (plane + 1) * 512],
+                in_=gws[plane][:],
+            )
+
+        prm = const.tile([P, 32], F32, name="prm")
+        prw = const.tile([P, 16], F32, name="prw")
+
+        def prep_params():
+            bank = tp.tile([P, 512], F32, name="tpp", tag="tp")
+            nc.tensor.transpose(out=bank[:, 0:128], in_=prn[:].bitcast(F32), identity=ident[:])
+            nc.vector.tensor_copy(out=prw[:], in_=bank[:, 0:16])
+            nc.vector.tensor_copy(out=prm[:], in_=prw[:].bitcast(BF16))
+
+        W_COL = {Z_PLANE: 0, R_PLANE: 4, G_PLANE: 16}
+        B_COL = {Z_PLANE: 8, R_PLANE: 12, G_PLANE: 20}
+
+        hbank = {}
+        gh = {}
+        hcod = {}
+        banks_r = {}
+        banks_z = {}
+        rr = {}
+        zz = {}
+        tt = {}
+        dq = {}
+        ghr = {}
+        hrcod = {}
+        flb = {}
+        ot = {}
+
+        def tr_h(j):
+            words = hn[j][:].bitcast(F32)
+            nsub = SIZES[j] // P
+            got = []
+            for first in range(0, nsub, 2):
+                subs = min(2, nsub - first)
+                bank = tp.tile([P, 512], F32, name="tph", tag="tp")
+                for sl in range(subs):
+                    for u in range(2):
+                        nc.tensor.transpose(
+                            out=bank[:, (u * subs + sl) * 128 : (u * subs + sl) * 128 + 128],
+                            in_=words[:, (first + sl) * 256 + u * 128 : (first + sl) * 256 + u * 128 + 128],
+                            identity=ident[:],
+                        )
+                got.append((bank, first, subs))
+            hbank[j] = got
+
+        def ev_h(j):
+            g = p4.tile([P, 2048], BF16, name="gh", tag="gh", align_bytes=64)
+            gwords = g[:].bitcast(F32)
+            for bank, first, subs in hbank[j]:
+                nc.scalar.copy(
+                    out=gwords[:, first * 256 : (first + subs) * 256].rearrange("p (n u) -> p n u", u=2),
+                    in_=bank[:, 0 : subs * 256].rearrange("p (u n) -> p n u", u=2),
+                )
+            gh[j] = g
+
+        def quantise(src, size, tagname):
+            c = p2.tile([P, 512], U32, name=tagname + "c", tag=tagname + "c", align_bytes=64)
+            s = p2.tile([P, 512], U8, name=tagname + "s", tag=tagname + "s", align_bytes=64)
+            nc.vector.quantize_mx(out=c[:, 0:size].bitcast(FP8X4), scales=s[:, 0:size], in_=src[:, 0 : 4 * size])
+            return (c, s)
+
+        def mx(plane, cs, size):
+            got = []
+            for t in range(4):
+                bank = mxp.tile([P, 512], F32, name="mx", tag="mx")
+                col = plane * 512 + t * 128
+                nc.tensor.matmul_mx(
+                    out=bank[:, 0:size],
+                    lhsT=wc[:, col : col + 128].bitcast(FP8X4),
+                    lhsT_scale=ws[:, col : col + 128],
+                    rhs=cs[0][:, 0:size].bitcast(FP8X4),
+                    rhs_scale=cs[1][:, 0:size],
+                    start=True,
+                    stop=True,
+                )
+                got.append(bank)
+            return got
+
+        def gate(j, plane, banks, dst, func):
+            size = SIZES[j]
+            nsub = size // P
+            xv = xb[:, starts[j] : starts[j] + size].rearrange("q (p s) -> q s p", s=nsub)
+            for t in range(4):
+                seg = dst[:, t * size : (t + 1) * size]
+                nc.vector.scalar_tensor_tensor(
+                    out=seg.rearrange("q (s p) -> q s p", s=nsub),
+                    in0=xv,
+                    scalar=prm[:, W_COL[plane] + t : W_COL[plane] + t + 1],
+                    in1=banks[t][:, 0:size].rearrange("q (s p) -> q s p", s=nsub),
+                    op0=ALU.mult,
+                    op1=ALU.add,
+                )
+                nc.scalar.activation(
+                    out=seg, in_=seg, func=func, bias=prm[:, B_COL[plane] + t : B_COL[plane] + t + 1], scale=1.0
+                )
+
+        def diff(eng, j, t0, t1):
+            size = SIZES[j]
+            eng.tensor_tensor(
+                out=dq[j][:, t0 * size : t1 * size].rearrange("p (t n) -> p t n", t=t1 - t0),
+                in0=gh[j][:, 0 : 4 * size].rearrange("p (n t) -> p t n", t=4)[:, t0:t1, :],
+                in1=tt[j][:, t0 * size : t1 * size].rearrange("p (t n) -> p t n", t=t1 - t0),
+                op=ALU.subtract,
+            )
+
+        def prod(eng, j, t0, t1):
+            size = SIZES[j]
+            cols = slice(t0 * size, t1 * size)
+            eng.tensor_tensor(out=dq[j][:, cols], in0=zz[j][:, cols], in1=dq[j][:, cols], op=ALU.mult)
+
+        def flip(j, s):
+            size = SIZES[j]
+            bank = flp.tile([P, 512], F32, name="fl", tag="fl")
+            for t in range(4):
+                lo = t * size + s * 128
+                o = bank[:, t * 128 : (t + 1) * 128]
+                nc.tensor.matmul(
+                    out=o, lhsT=dq[j][:, lo : lo + 128], rhs=ident[:], is_transpose=True, start=True, stop=False
+                )
+                nc.tensor.matmul(
+                    out=o, lhsT=tt[j][:, lo : lo + 128], rhs=ident[:], is_transpose=True, start=False, stop=True
+                )
+            flb[(j, s)] = bank
+
+        def ev_out(j, s):
+            nc.scalar.copy(
+                out=ot[j][:, s * 512 : (s + 1) * 512].rearrange("b (u p e) -> b u p e", u=2, e=2),
+                in_=flb[(j, s)][:].rearrange("b (u e p) -> b u p e", u=2, e=2),
+            )
+
+        def finish(j):
+            size = SIZES[j]
+            nsub = size // P
+            otile = p2.tile([P, 2048], F32, name="ot", tag="ot")
+            ot[j] = otile
+            for s in range(nsub):
+                flip(j, s)
+                if s >= 1:
+                    ev_out(j, s - 1)
+            ev_out(j, nsub - 1)
+            nc.sync.dma_start(
+                out=out[starts[j] : starts[j] + size, :].rearrange("(p s) c -> p (s c)", s=nsub),
+                in_=otile[:, 0 : nsub * 512],
+            )
+
+        def ok(j):
+            return 0 <= j < nblk
+
+        prep_w_tr(R_PLANE, "vs")
+        tr_h(0)
+        ev_h(0)
+        prep_w_q(R_PLANE)
+        prep_params()
+        hcod[0] = quantise(gh[0], SIZES[0], "h")
+        banks_r[0] = mx(R_PLANE, hcod[0], SIZES[0])
+        tr_h(1)
+        ev_h(1)
+        prep_w_tr(Z_PLANE, "ss")
+        for i in range(0, nblk + 3):
+            if ok(i):
+                rtile = p2.tile([P, 2048], F32, name="rr", tag="rr")
+                rr[i] = rtile
+                gate(i, R_PLANE, banks_r[i], rtile, ACT.Sigmoid)
+            if i == 0:
+                prep_w_q(Z_PLANE)
+            if ok(i - 1):
+                j = i - 1
+                ttile = p3.tile([P, 2048], F32, name="tt", tag="tt")
+                tt[j] = ttile
+                gate(j, G_PLANE, mx(G_PLANE, hrcod[j], SIZES[j]), ttile, ACT.Tanh)
+                dtile = p3.tile([P, 2048], F32, name="dq", tag="dq")
+                dq[j] = dtile
+                if j >= nblk - V_TAIL:
+                    for t in range(4):
+                        diff(nc.vector, j, t, t + 1)
+                        prod(nc.vector, j, t, t + 1)
+                else:
+                    diff(nc.gpsimd, j, 2, 4)
+                    diff(nc.gpsimd, j, 0, 2)
+                    prod(nc.gpsimd, j, 0, 2)
+            if ok(i):
+                banks_z[i] = mx(Z_PLANE, hcod[i], SIZES[i])
+            if ok(i - 3):
+                finish(i - 3)
+            if ok(i + 2):
+                tr_h(i + 2)
+                ev_h(i + 2)
+            if i == 0:
+                prep_w_tr(G_PLANE, "ss")
+            if ok(i):
+                hrt = p2.tile([P, 2048], BF16, name="ghr", tag="ghr", align_bytes=64)
+                ghr[i] = hrt
+                size = SIZES[i]
+                nc.vector.tensor_tensor(
+                    out=hrt[:, 0 : 4 * size].rearrange("p (n t) -> p n t", t=4),
+                    in0=rr[i][:, 0 : 4 * size].rearrange("p (t n) -> p n t", t=4),
+                    in1=gh[i][:, 0 : 4 * size].rearrange("p (n t) -> p n t", t=4),
+                    op=ALU.mult,
+                )
+            if ok(i - 2) and i - 2 < nblk - V_TAIL:
+                prod(nc.vector, i - 2, 2, 4)
+            if ok(i):
+                hrcod[i] = quantise(ghr[i], SIZES[i], "r")
+            if ok(i + 1):
+                hcod[i + 1] = quantise(gh[i + 1], SIZES[i + 1], "h")
+            if ok(i):
+                ztile = p3.tile([P, 2048], F32, name="zz", tag="zz")
+                zz[i] = ztile
+                gate(i, Z_PLANE, banks_z[i], ztile, ACT.Sigmoid)
+            if i == 0:
+                prep_w_q(G_PLANE)
+            if ok(i + 1):
+                banks_r[i + 1] = mx(R_PLANE, hcod[i + 1], SIZES[i + 1])

@@ -22,6 +22,7 @@ G_PLANE = 2
 PINNED = True
 SIZES = [256, 512, 512, 512, 512, 512, 512, 512, 128, 128]
 V_TAIL = 2
+G_Q_T = 0
 X_FIRST = SIZES[0] + SIZES[1]
 assert sum(SIZES) == B
 
@@ -264,6 +265,8 @@ def tile_grucell_t_kernel(
                 in_=otile[:, 0 : nsub * 512],
             )
 
+        scr = const.tile([P, 2], F32, name="scr")
+
         def ok(j):
             return 0 <= j < nblk
 
@@ -295,10 +298,6 @@ def tile_grucell_t_kernel(
                     for t in range(4):
                         diff(nc.vector, j, t, t + 1)
                         prod(nc.vector, j, t, t + 1)
-                else:
-                    diff(nc.gpsimd, j, 2, 4)
-                    diff(nc.gpsimd, j, 0, 2)
-                    prod(nc.gpsimd, j, 0, 2)
             if ok(i):
                 banks_z[i] = mx(Z_PLANE, hcod[i], SIZES[i])
             if ok(i - 3):
@@ -318,12 +317,21 @@ def tile_grucell_t_kernel(
                     in1=gh[i][:, 0 : 4 * size].rearrange("p (n t) -> p n t", t=4),
                     op=ALU.mult,
                 )
-            if ok(i - 2) and i - 2 < nblk - V_TAIL:
-                prod(nc.vector, i - 2, 2, 4)
-            if ok(i):
-                hrcod[i] = quantise(ghr[i], SIZES[i], "r")
             if ok(i + 1):
                 hcod[i + 1] = quantise(gh[i + 1], SIZES[i + 1], "h")
+            if ok(i):
+                hrcod[i] = quantise(ghr[i], SIZES[i], "r")
+            if ok(i - 2) and i - 2 < nblk - V_TAIL:
+                prod(nc.vector, i - 2, G_Q_T, 4)
+            if ok(i - 1) and i - 1 < nblk - V_TAIL:
+                if ok(i - 2) and i - 2 < nblk - V_TAIL:
+                    nc.gpsimd.tensor_copy(out=scr[:, 0:1], in_=dq[i - 2][:, 4 * SIZES[i - 2] - 1 : 4 * SIZES[i - 2]])
+                elif ok(i):
+                    nc.gpsimd.tensor_copy(out=scr[:, 0:1], in_=ghr[i][:, 4 * SIZES[i] - 1 : 4 * SIZES[i]])
+                diff(nc.gpsimd, i - 1, 2, 4)
+                diff(nc.gpsimd, i - 1, 0, 2)
+                if G_Q_T > 0:
+                    prod(nc.gpsimd, i - 1, 0, G_Q_T)
             if ok(i):
                 ztile = p3.tile([P, 2048], F32, name="zz", tag="zz")
                 zz[i] = ztile

@@ -21,7 +21,7 @@ R_PLANE = 1
 G_PLANE = 2
 PINNED = True
 SIZES = [256, 512, 512, 512, 512, 512, 512, 512, 128, 128]
-V_TAIL = 2
+V_TAIL = 10
 G_Q_T = 0
 X_FIRST = SIZES[0] + SIZES[1]
 assert sum(SIZES) == B

@@ -20,8 +20,8 @@ Z_PLANE = 0
 R_PLANE = 1
 G_PLANE = 2
 PINNED = True
-SIZES = [256, 512, 512, 512, 512, 512, 512, 512, 128, 128]
-V_TAIL = 10
+SIZES = [512, 512, 512, 512, 512, 512, 512, 512]
+V_TAIL = 1
 G_Q_T = 0
 X_FIRST = SIZES[0] + SIZES[1]
 assert sum(SIZES) == B
@@ -198,7 +198,7 @@ def tile_grucell_t_kernel(
                 got.append(bank)
             return got
 
-        def gate(j, plane, banks, dst, func):
+        def gate(j, plane, banks, dst, func, q2):
             size = SIZES[j]
             nsub = size // P
             xv = xb[:, starts[j] : starts[j] + size].rearrange("q (p s) -> q s p", s=nsub)
@@ -215,6 +215,8 @@ def tile_grucell_t_kernel(
                 nc.scalar.activation(
                     out=seg, in_=seg, func=func, bias=prm[:, B_COL[plane] + t : B_COL[plane] + t + 1], scale=1.0
                 )
+                if t == 0 and q2 is not None:
+                    hrcod[q2] = quantise(ghr[q2], SIZES[q2], "r")
 
         def diff(eng, j, t0, t1):
             size = SIZES[j]
@@ -265,11 +267,37 @@ def tile_grucell_t_kernel(
                 in_=otile[:, 0 : nsub * 512],
             )
 
-        scr = const.tile([P, 2], F32, name="scr")
-
         def ok(j):
             return 0 <= j < nblk
 
+        def rows_view(tile_ap, j, s):
+            size = SIZES[j]
+            return tile_ap[:, 0 : 4 * size].rearrange("p (t n) -> p t n", t=4)[:, :, s * 128 : (s + 1) * 128]
+
+        def diff_rows(j, s):
+            size = SIZES[j]
+            nc.vector.tensor_tensor(
+                out=rows_view(dq[j], j, s),
+                in0=gh[j][:, 0 : 4 * size].rearrange("p (n t) -> p t n", t=4)[:, :, s * 128 : (s + 1) * 128],
+                in1=rows_view(tt[j], j, s),
+                op=ALU.subtract,
+            )
+
+        def prod_rows(j, s):
+            nc.vector.tensor_tensor(
+                out=rows_view(dq[j], j, s), in0=rows_view(zz[j], j, s), in1=rows_view(dq[j], j, s), op=ALU.mult
+            )
+
+        def finish_rows(j, s):
+            size = SIZES[j]
+            flip(j, s)
+            ev_out(j, s)
+            nc.sync.dma_start(
+                out=out[starts[j] : starts[j] + size, :].rearrange("(p s) c -> p s c", s=size // P)[:, s, :],
+                in_=ot[j][:, s * 512 : (s + 1) * 512],
+            )
+
+        last = nblk - 1
         prep_w_tr(R_PLANE, "vs")
         tr_h(0)
         ev_h(0)
@@ -280,62 +308,59 @@ def tile_grucell_t_kernel(
         tr_h(1)
         ev_h(1)
         prep_w_tr(Z_PLANE, "ss")
-        for i in range(0, nblk + 3):
+        for i in range(0, nblk + 2):
             if ok(i):
                 rtile = p2.tile([P, 2048], F32, name="rr", tag="rr")
                 rr[i] = rtile
-                gate(i, R_PLANE, banks_r[i], rtile, ACT.Sigmoid)
+                gate(i, R_PLANE, banks_r[i], rtile, ACT.Sigmoid, None)
             if i == 0:
                 prep_w_q(Z_PLANE)
             if ok(i - 1):
                 j = i - 1
-                ttile = p3.tile([P, 2048], F32, name="tt", tag="tt")
+                ttile = p2.tile([P, 2048], F32, name="tt", tag="tt")
                 tt[j] = ttile
-                gate(j, G_PLANE, mx(G_PLANE, hrcod[j], SIZES[j]), ttile, ACT.Tanh)
-                dtile = p3.tile([P, 2048], F32, name="dq", tag="dq")
+                gate(j, G_PLANE, mx(G_PLANE, hrcod[j], SIZES[j]), ttile, ACT.Tanh, None)
+                dtile = p2.tile([P, 2048], F32, name="dq", tag="dq")
                 dq[j] = dtile
-                if j >= nblk - V_TAIL:
+                if j != last:
                     for t in range(4):
-                        diff(nc.vector, j, t, t + 1)
-                        prod(nc.vector, j, t, t + 1)
+                        diff(nc.gpsimd, j, t, t + 1)
             if ok(i):
                 banks_z[i] = mx(Z_PLANE, hcod[i], SIZES[i])
-            if ok(i - 3):
-                finish(i - 3)
+            if ok(i - 2) and i - 2 != last:
+                prod(nc.vector, i - 2, 0, 4)
             if ok(i + 2):
                 tr_h(i + 2)
                 ev_h(i + 2)
             if i == 0:
                 prep_w_tr(G_PLANE, "ss")
+            if ok(i - 2) and i - 2 != last:
+                finish(i - 2)
+            if i - 1 == last:
+                nsub = SIZES[last] // P
+                otile = p2.tile([P, 2048], F32, name="ot", tag="ot")
+                ot[last] = otile
+                diff_rows(last, 0)
+                for s in range(nsub):
+                    if s + 1 < nsub:
+                        diff_rows(last, s + 1)
+                    prod_rows(last, s)
+                    finish_rows(last, s)
+            if ok(i + 1):
+                hcod[i + 1] = quantise(gh[i + 1], SIZES[i + 1], "h")
             if ok(i):
                 hrt = p2.tile([P, 2048], BF16, name="ghr", tag="ghr", align_bytes=64)
                 ghr[i] = hrt
                 size = SIZES[i]
                 nc.vector.tensor_tensor(
-                    out=hrt[:, 0 : 4 * size].rearrange("p (n t) -> p n t", t=4),
-                    in0=rr[i][:, 0 : 4 * size].rearrange("p (t n) -> p n t", t=4),
-                    in1=gh[i][:, 0 : 4 * size].rearrange("p (n t) -> p n t", t=4),
+                    out=hrt[:, 0 : 4 * size].rearrange("p (c k t) -> p c t k", k=4, t=4),
+                    in0=rr[i][:, 0 : 4 * size].rearrange("p (t c k) -> p c t k", k=4, t=4),
+                    in1=gh[i][:, 0 : 4 * size].rearrange("p (c k t) -> p c t k", k=4, t=4),
                     op=ALU.mult,
                 )
-            if ok(i + 1):
-                hcod[i + 1] = quantise(gh[i + 1], SIZES[i + 1], "h")
-            if ok(i):
-                hrcod[i] = quantise(ghr[i], SIZES[i], "r")
-            if ok(i - 2) and i - 2 < nblk - V_TAIL:
-                prod(nc.vector, i - 2, G_Q_T, 4)
-            if ok(i - 1) and i - 1 < nblk - V_TAIL:
-                if ok(i - 2) and i - 2 < nblk - V_TAIL:
-                    nc.gpsimd.tensor_copy(out=scr[:, 0:1], in_=dq[i - 2][:, 4 * SIZES[i - 2] - 1 : 4 * SIZES[i - 2]])
-                elif ok(i):
-                    nc.gpsimd.tensor_copy(out=scr[:, 0:1], in_=ghr[i][:, 4 * SIZES[i] - 1 : 4 * SIZES[i]])
-                diff(nc.gpsimd, i - 1, 2, 4)
-                diff(nc.gpsimd, i - 1, 0, 2)
-                if G_Q_T > 0:
-                    prod(nc.gpsimd, i - 1, 0, G_Q_T)
-            if ok(i):
                 ztile = p3.tile([P, 2048], F32, name="zz", tag="zz")
                 zz[i] = ztile
-                gate(i, Z_PLANE, banks_z[i], ztile, ACT.Sigmoid)
+                gate(i, Z_PLANE, banks_z[i], ztile, ACT.Sigmoid, i)
             if i == 0:
                 prep_w_q(G_PLANE)
             if ok(i + 1):

@@ -22,7 +22,7 @@ G_PLANE = 2
 PINNED = True
 SIZES = [512, 512, 512, 512, 512, 512, 512, 512]
 V_TAIL = 1
-G_Q_T = 0
+G_Q_T = 2
 X_FIRST = SIZES[0] + SIZES[1]
 assert sum(SIZES) == B
 
@@ -323,17 +323,15 @@ def tile_grucell_t_kernel(
                 dtile = p2.tile([P, 2048], F32, name="dq", tag="dq")
                 dq[j] = dtile
                 if j != last:
-                    for t in range(4):
+                    for t in (3, 2, 1, 0):
                         diff(nc.gpsimd, j, t, t + 1)
+                    for t in range(G_Q_T):
+                        prod(nc.gpsimd, j, t, t + 1)
             if ok(i):
                 banks_z[i] = mx(Z_PLANE, hcod[i], SIZES[i])
+                tr_h(i)
             if ok(i - 2) and i - 2 != last:
-                prod(nc.vector, i - 2, 0, 4)
-            if ok(i + 2):
-                tr_h(i + 2)
-                ev_h(i + 2)
-            if i == 0:
-                prep_w_tr(G_PLANE, "ss")
+                prod(nc.vector, i - 2, G_Q_T, 4)
             if ok(i - 2) and i - 2 != last:
                 finish(i - 2)
             if i - 1 == last:
@@ -352,12 +350,21 @@ def tile_grucell_t_kernel(
                 hrt = p2.tile([P, 2048], BF16, name="ghr", tag="ghr", align_bytes=64)
                 ghr[i] = hrt
                 size = SIZES[i]
-                nc.vector.tensor_tensor(
-                    out=hrt[:, 0 : 4 * size].rearrange("p (c k t) -> p c t k", k=4, t=4),
-                    in0=rr[i][:, 0 : 4 * size].rearrange("p (t c k) -> p c t k", k=4, t=4),
-                    in1=gh[i][:, 0 : 4 * size].rearrange("p (c k t) -> p c t k", k=4, t=4),
-                    op=ALU.mult,
-                )
+                for bank, first, subs in hbank[i]:
+                    nc.vector.tensor_tensor(
+                        out=hrt[:, first * 512 : (first + subs) * 512].rearrange("p (n u e) -> p n u e", u=2, e=2),
+                        in0=rr[i][:, 0 : 4 * size].rearrange("p (u e n) -> p n u e", u=2, e=2)[
+                            :, first * 128 : (first + subs) * 128, :, :
+                        ],
+                        in1=bank[:, 0 : subs * 256].bitcast(BF16).rearrange("p (u n e) -> p n u e", u=2, e=2),
+                        op=ALU.mult,
+                    )
+            if ok(i + 2):
+                tr_h(i + 2)
+                ev_h(i + 2)
+            if i == 0:
+                prep_w_tr(G_PLANE, "ss")
+            if ok(i):
                 ztile = p3.tile([P, 2048], F32, name="zz", tag="zz")
                 zz[i] = ztile
                 gate(i, Z_PLANE, banks_z[i], ztile, ACT.Sigmoid, i)

@@ -94,12 +94,12 @@ def tile_grucell_t_kernel(
         ws = const.tile([P, 3 * 512], U8, name="ws", align_bytes=64)
         gws = {}
 
-        def prep_w_tr(plane, engines):
+        def prep_w_tr(plane, engines, pool, tagname):
             words = wn[plane][:].bitcast(F32)
             gw = const.tile([P, 2048], BF16, name="gw%d" % plane, align_bytes=64)
             gww = gw[:].bitcast(F32)
             for u in range(2):
-                bank = tp.tile([P, 512], F32, name="tpw", tag="tp")
+                bank = pool.tile([P, 512], F32, name="tpw", tag=tagname)
                 for e in range(2):
                     for kh in range(2):
                         nc.tensor.transpose(
@@ -122,7 +122,10 @@ def tile_grucell_t_kernel(
                 in_=gws[plane][:],
             )
 
+        identb = const.tile([P, P], BF16, name="identb")
+        make_identity(nc, identb[:])
         prm = const.tile([P, 32], F32, name="prm")
+        nbz = const.tile([P, 4], F32, name="nbz")
         prw = const.tile([P, 16], F32, name="prw")
 
         def prep_params():
@@ -130,6 +133,7 @@ def tile_grucell_t_kernel(
             nc.tensor.transpose(out=bank[:, 0:128], in_=prn[:].bitcast(F32), identity=ident[:])
             nc.vector.tensor_copy(out=prw[:], in_=bank[:, 0:16])
             nc.vector.tensor_copy(out=prm[:], in_=prw[:].bitcast(BF16))
+            nc.vector.tensor_scalar_mul(out=nbz[:], in0=prm[:, 8:12], scalar1=-1.0)
 
         W_COL = {Z_PLANE: 0, R_PLANE: 4, G_PLANE: 16}
         B_COL = {Z_PLANE: 8, R_PLANE: 12, G_PLANE: 20}
@@ -212,9 +216,12 @@ def tile_grucell_t_kernel(
                     op0=ALU.mult,
                     op1=ALU.add,
                 )
-                nc.scalar.activation(
-                    out=seg, in_=seg, func=func, bias=prm[:, B_COL[plane] + t : B_COL[plane] + t + 1], scale=1.0
-                )
+                if plane == Z_PLANE:
+                    nc.scalar.activation(out=seg, in_=seg, func=func, bias=nbz[:, t : t + 1], scale=-1.0)
+                else:
+                    nc.scalar.activation(
+                        out=seg, in_=seg, func=func, bias=prm[:, B_COL[plane] + t : B_COL[plane] + t + 1], scale=1.0
+                    )
                 if t == 0 and q2 is not None:
                     hrcod[q2] = quantise(ghr[q2], SIZES[q2], "r")
 
@@ -222,8 +229,8 @@ def tile_grucell_t_kernel(
             size = SIZES[j]
             eng.tensor_tensor(
                 out=dq[j][:, t0 * size : t1 * size].rearrange("p (t n) -> p t n", t=t1 - t0),
-                in0=gh[j][:, 0 : 4 * size].rearrange("p (n t) -> p t n", t=4)[:, t0:t1, :],
-                in1=tt[j][:, t0 * size : t1 * size].rearrange("p (t n) -> p t n", t=t1 - t0),
+                in0=tt[j][:, t0 * size : t1 * size].rearrange("p (t n) -> p t n", t=t1 - t0),
+                in1=gh[j][:, 0 : 4 * size].rearrange("p (n t) -> p t n", t=4)[:, t0:t1, :],
                 op=ALU.subtract,
             )
 
@@ -235,14 +242,22 @@ def tile_grucell_t_kernel(
         def flip(j, s):
             size = SIZES[j]
             bank = flp.tile([P, 512], F32, name="fl", tag="fl")
+            nc.tensor.matmul(
+                out=bank[:],
+                lhsT=identb[:],
+                rhs=hn[j][:, s * 512 : (s + 1) * 512].rearrange("b (u p e) -> b u e p", u=2, e=2),
+                start=True,
+                stop=False,
+            )
             for t in range(4):
                 lo = t * size + s * 128
-                o = bank[:, t * 128 : (t + 1) * 128]
                 nc.tensor.matmul(
-                    out=o, lhsT=dq[j][:, lo : lo + 128], rhs=ident[:], is_transpose=True, start=True, stop=False
-                )
-                nc.tensor.matmul(
-                    out=o, lhsT=tt[j][:, lo : lo + 128], rhs=ident[:], is_transpose=True, start=False, stop=True
+                    out=bank[:, t * 128 : (t + 1) * 128],
+                    lhsT=dq[j][:, lo : lo + 128],
+                    rhs=ident[:],
+                    is_transpose=True,
+                    start=False,
+                    stop=(t == 3),
                 )
             flb[(j, s)] = bank
 
@@ -252,15 +267,19 @@ def tile_grucell_t_kernel(
                 in_=flb[(j, s)][:].rearrange("b (u e p) -> b u p e", u=2, e=2),
             )
 
-        def finish(j):
+        def finish_a(j):
+            flip(j, 0)
+            flip(j, 1)
+
+        def finish_b(j):
             size = SIZES[j]
             nsub = size // P
             otile = p2.tile([P, 2048], F32, name="ot", tag="ot")
             ot[j] = otile
-            for s in range(nsub):
+            for s in range(2, nsub):
+                ev_out(j, s - 2)
                 flip(j, s)
-                if s >= 1:
-                    ev_out(j, s - 1)
+            ev_out(j, nsub - 2)
             ev_out(j, nsub - 1)
             nc.sync.dma_start(
                 out=out[starts[j] : starts[j] + size, :].rearrange("(p s) c -> p (s c)", s=nsub),
@@ -278,8 +297,8 @@ def tile_grucell_t_kernel(
             size = SIZES[j]
             nc.vector.tensor_tensor(
                 out=rows_view(dq[j], j, s),
-                in0=gh[j][:, 0 : 4 * size].rearrange("p (n t) -> p t n", t=4)[:, :, s * 128 : (s + 1) * 128],
-                in1=rows_view(tt[j], j, s),
+                in0=rows_view(tt[j], j, s),
+                in1=gh[j][:, 0 : 4 * size].rearrange("p (n t) -> p t n", t=4)[:, :, s * 128 : (s + 1) * 128],
                 op=ALU.subtract,
             )
 
@@ -298,77 +317,104 @@ def tile_grucell_t_kernel(
             )
 
         last = nblk - 1
-        prep_w_tr(R_PLANE, "vs")
+        banks_g = {}
+
+        def gates_r(i):
+            rtile = p2.tile([P, 2048], F32, name="rr", tag="rr")
+            rr[i] = rtile
+            gate(i, R_PLANE, banks_r[i], rtile, ACT.Sigmoid, None)
+
+        def gates_g(j):
+            ttile = p2.tile([P, 2048], F32, name="tt", tag="tt")
+            tt[j] = ttile
+            gate(j, G_PLANE, banks_g[j], ttile, ACT.Tanh, None)
+            dtile = p2.tile([P, 2048], F32, name="dq", tag="dq")
+            dq[j] = dtile
+            if j != last:
+                for t in (3, 2, 1, 0):
+                    diff(nc.gpsimd, j, t, t + 1)
+                for t in range(G_Q_T):
+                    prod(nc.gpsimd, j, t, t + 1)
+
+        def gates_z(i):
+            ztile = p3.tile([P, 2048], F32, name="zz", tag="zz")
+            zz[i] = ztile
+            gate(i, Z_PLANE, banks_z[i], ztile, ACT.Sigmoid, i)
+
+        def h_times_r(i):
+            hrt = p2.tile([P, 2048], BF16, name="ghr", tag="ghr", align_bytes=64)
+            ghr[i] = hrt
+            size = SIZES[i]
+            for bank, first, subs in hbank[i]:
+                nc.vector.tensor_tensor(
+                    out=hrt[:, first * 512 : (first + subs) * 512].rearrange("p (n u e) -> p n u e", u=2, e=2),
+                    in0=rr[i][:, 0 : 4 * size].rearrange("p (u e n) -> p n u e", u=2, e=2)[
+                        :, first * 128 : (first + subs) * 128, :, :
+                    ],
+                    in1=bank[:, 0 : subs * 256].bitcast(BF16).rearrange("p (u n e) -> p n u e", u=2, e=2),
+                    op=ALU.mult,
+                )
+
+        def last_block():
+            nsub = SIZES[last] // P
+            otile = p2.tile([P, 2048], F32, name="ot", tag="ot")
+            ot[last] = otile
+            diff_rows(last, 0)
+            for s in range(nsub):
+                if s + 1 < nsub:
+                    diff_rows(last, s + 1)
+                prod_rows(last, s)
+                finish_rows(last, s)
+
+        prep_w_tr(R_PLANE, "vs", tp, "tp")
         tr_h(0)
         ev_h(0)
         prep_w_q(R_PLANE)
         prep_params()
+        prep_w_tr(Z_PLANE, "ss", flp, "fl")
         hcod[0] = quantise(gh[0], SIZES[0], "h")
         banks_r[0] = mx(R_PLANE, hcod[0], SIZES[0])
+
+        gates_r(0)
+        prep_w_q(Z_PLANE)
+        tr_h(0)
+        prep_w_tr(G_PLANE, "ss", flp, "fl")
+        banks_z[0] = mx(Z_PLANE, hcod[0], SIZES[0])
+        h_times_r(0)
         tr_h(1)
         ev_h(1)
-        prep_w_tr(Z_PLANE, "ss")
-        for i in range(0, nblk + 2):
-            if ok(i):
-                rtile = p2.tile([P, 2048], F32, name="rr", tag="rr")
-                rr[i] = rtile
-                gate(i, R_PLANE, banks_r[i], rtile, ACT.Sigmoid, None)
-            if i == 0:
-                prep_w_q(Z_PLANE)
-            if ok(i - 1):
-                j = i - 1
-                ttile = p2.tile([P, 2048], F32, name="tt", tag="tt")
-                tt[j] = ttile
-                gate(j, G_PLANE, mx(G_PLANE, hrcod[j], SIZES[j]), ttile, ACT.Tanh, None)
-                dtile = p2.tile([P, 2048], F32, name="dq", tag="dq")
-                dq[j] = dtile
-                if j != last:
-                    for t in (3, 2, 1, 0):
-                        diff(nc.gpsimd, j, t, t + 1)
-                    for t in range(G_Q_T):
-                        prod(nc.gpsimd, j, t, t + 1)
-            if ok(i):
-                banks_z[i] = mx(Z_PLANE, hcod[i], SIZES[i])
-                tr_h(i)
-            if ok(i - 2) and i - 2 != last:
+        gates_z(0)
+        hcod[1] = quantise(gh[1], SIZES[1], "h")
+        prep_w_q(G_PLANE)
+        banks_r[1] = mx(R_PLANE, hcod[1], SIZES[1])
+        tr_h(2)
+        ev_h(2)
+
+        for i in range(1, nblk):
+            gates_r(i)
+            banks_g[i - 1] = mx(G_PLANE, hrcod[i - 1], SIZES[i - 1])
+            if i >= 2:
                 prod(nc.vector, i - 2, G_Q_T, 4)
-            if ok(i - 2) and i - 2 != last:
-                finish(i - 2)
-            if i - 1 == last:
-                nsub = SIZES[last] // P
-                otile = p2.tile([P, 2048], F32, name="ot", tag="ot")
-                ot[last] = otile
-                diff_rows(last, 0)
-                for s in range(nsub):
-                    if s + 1 < nsub:
-                        diff_rows(last, s + 1)
-                    prod_rows(last, s)
-                    finish_rows(last, s)
-            if ok(i + 1):
+            tr_h(i)
+            if i >= 2:
+                finish_a(i - 2)
+            gates_g(i - 1)
+            banks_z[i] = mx(Z_PLANE, hcod[i], SIZES[i])
+            if i >= 2:
+                finish_b(i - 2)
+            if i + 1 < nblk:
                 hcod[i + 1] = quantise(gh[i + 1], SIZES[i + 1], "h")
-            if ok(i):
-                hrt = p2.tile([P, 2048], BF16, name="ghr", tag="ghr", align_bytes=64)
-                ghr[i] = hrt
-                size = SIZES[i]
-                for bank, first, subs in hbank[i]:
-                    nc.vector.tensor_tensor(
-                        out=hrt[:, first * 512 : (first + subs) * 512].rearrange("p (n u e) -> p n u e", u=2, e=2),
-                        in0=rr[i][:, 0 : 4 * size].rearrange("p (u e n) -> p n u e", u=2, e=2)[
-                            :, first * 128 : (first + subs) * 128, :, :
-                        ],
-                        in1=bank[:, 0 : subs * 256].bitcast(BF16).rearrange("p (u n e) -> p n u e", u=2, e=2),
-                        op=ALU.mult,
-                    )
-            if ok(i + 2):
+            h_times_r(i)
+            if i + 2 < nblk:
                 tr_h(i + 2)
                 ev_h(i + 2)
-            if i == 0:
-                prep_w_tr(G_PLANE, "ss")
-            if ok(i):
-                ztile = p3.tile([P, 2048], F32, name="zz", tag="zz")
-                zz[i] = ztile
-                gate(i, Z_PLANE, banks_z[i], ztile, ACT.Sigmoid, i)
-            if i == 0:
-                prep_w_q(G_PLANE)
-            if ok(i + 1):
+            gates_z(i)
+            if i + 1 < nblk:
                 banks_r[i + 1] = mx(R_PLANE, hcod[i + 1], SIZES[i + 1])
+
+        banks_g[last] = mx(G_PLANE, hrcod[last], SIZES[last])
+        gates_g(last)
+        prod(nc.vector, last - 1, G_Q_T, 4)
+        finish_a(last - 1)
+        finish_b(last - 1)
+        last_block()

@@ -22,7 +22,7 @@ G_PLANE = 2
 PINNED = True
 SIZES = [512, 512, 512, 512, 512, 512, 512, 512]
 V_TAIL = 1
-G_Q_T = 2
+G_Q_T = 3
 X_FIRST = SIZES[0] + SIZES[1]
 assert sum(SIZES) == B
 
@@ -89,6 +89,18 @@ def tile_grucell_t_kernel(
         nc.sync.dma_start(out=xb[:, X_FIRST:B], in_=xrow[X_FIRST:B].partition_broadcast(P))
         for j in range(3, nblk):
             load_h(nc.sync, j)
+
+        xp = const.tile([P, B], BF16, name="xp")
+        for j in range(nblk):
+            cols = slice(starts[j], starts[j] + SIZES[j])
+            nc.gpsimd.tensor_scalar(
+                out=xp[:, cols].rearrange("q (s p) -> q s p", s=SIZES[j] // P),
+                in0=xb[:, cols].rearrange("q (p s) -> q s p", s=SIZES[j] // P),
+                scalar1=1.0,
+                scalar2=0.0,
+                op0=ALU.mult,
+                op1=ALU.add,
+            )
 
         wc = const.tile([P, 3 * 512], U32, name="wc", align_bytes=64)
         ws = const.tile([P, 3 * 512], U8, name="ws", align_bytes=64)
@@ -205,14 +217,14 @@ def tile_grucell_t_kernel(
         def gate(j, plane, banks, dst, func, q2):
             size = SIZES[j]
             nsub = size // P
-            xv = xb[:, starts[j] : starts[j] + size].rearrange("q (p s) -> q s p", s=nsub)
+            xv = xp[:, starts[j] : starts[j] + size]
             for t in range(4):
                 seg = dst[:, t * size : (t + 1) * size]
                 nc.vector.scalar_tensor_tensor(
-                    out=seg.rearrange("q (s p) -> q s p", s=nsub),
+                    out=seg,
                     in0=xv,
                     scalar=prm[:, W_COL[plane] + t : W_COL[plane] + t + 1],
-                    in1=banks[t][:, 0:size].rearrange("q (s p) -> q s p", s=nsub),
+                    in1=banks[t][:, 0:size],
                     op0=ALU.mult,
                     op1=ALU.add,
                 )
@@ -319,6 +331,9 @@ def tile_grucell_t_kernel(
         last = nblk - 1
         banks_g = {}
 
+        def g_share(j):
+            return G_Q_T if j < last - 1 else 2
+
         def gates_r(i):
             rtile = p2.tile([P, 2048], F32, name="rr", tag="rr")
             rr[i] = rtile
@@ -333,7 +348,7 @@ def tile_grucell_t_kernel(
             if j != last:
                 for t in (3, 2, 1, 0):
                     diff(nc.gpsimd, j, t, t + 1)
-                for t in range(G_Q_T):
+                for t in range(g_share(j)):
                     prod(nc.gpsimd, j, t, t + 1)
 
         def gates_z(i):
@@ -394,7 +409,7 @@ def tile_grucell_t_kernel(
             gates_r(i)
             banks_g[i - 1] = mx(G_PLANE, hrcod[i - 1], SIZES[i - 1])
             if i >= 2:
-                prod(nc.vector, i - 2, G_Q_T, 4)
+                prod(nc.vector, i - 2, g_share(i - 2), 4)
             tr_h(i)
             if i >= 2:
                 finish_a(i - 2)
@@ -414,7 +429,7 @@ def tile_grucell_t_kernel(
 
         banks_g[last] = mx(G_PLANE, hrcod[last], SIZES[last])
         gates_g(last)
-        prod(nc.vector, last - 1, G_Q_T, 4)
+        prod(nc.vector, last - 1, g_share(last - 1), 4)
         finish_a(last - 1)
         finish_b(last - 1)
         last_block()

@@ -14,36 +14,30 @@ ACT = mybir.ActivationFunctionType
 P = 128
 B = 4096
 D = 512
+N = 512
+NSUB = N // P
+NBLK = B // N
+LAST = NBLK - 1
 FLOPS = 2 * B * D * 3 * D
 
-Z_PLANE = 0
-R_PLANE = 1
+R_PLANE = 0
+Z_PLANE = 1
 G_PLANE = 2
-PINNED = True
-SIZES = [512, 512, 512, 512, 512, 512, 512, 512]
-V_TAIL = 1
-G_Q_T = 3
-X_FIRST = SIZES[0] + SIZES[1]
-assert sum(SIZES) == B
+X_FIRST = 2 * N
 
 
 def tile_grucell_t_kernel(
     tc, inputs, hidden, gate_w_I2H, gate_w_H2H, gate_bias, update_w_I2H, update_w_H2H, update_bias, out
 ):
     nc = tc.nc
-    nblk = len(SIZES)
-    starts = [sum(SIZES[:j]) for j in range(nblk)]
     with ExitStack() as ctx:
         const = ctx.enter_context(tc.tile_pool(name="const", bufs=1))
-        hpool = ctx.enter_context(tc.tile_pool(name="hpool", bufs=nblk))
+        hpool = ctx.enter_context(tc.tile_pool(name="hpool", bufs=NBLK))
         p2 = ctx.enter_context(tc.tile_pool(name="p2", bufs=2))
         p3 = ctx.enter_context(tc.tile_pool(name="p3", bufs=3))
-        p4 = ctx.enter_context(tc.tile_pool(name="p4", bufs=4))
-        tp = ctx.enter_context(tc.psum_pool(name="tp", bufs=2))
         mxp = ctx.enter_context(tc.psum_pool(name="mxp", bufs=4))
-        flp = ctx.enter_context(tc.psum_pool(name="flp", bufs=2))
-        if PINNED:
-            ctx.enter_context(tc.manual_schedule())
+        flp = ctx.enter_context(tc.psum_pool(name="flp", bufs=4))
+        ctx.enter_context(tc.manual_schedule())
 
         ident = const.tile([P, P], F32, name="ident")
         make_identity(nc, ident[:])
@@ -58,18 +52,23 @@ def tile_grucell_t_kernel(
 
         def load_w(plane, rows):
             wnat = const.tile([P, 2048], BF16, name="wn%d" % plane)
-            nc.sync.dma_start(
-                out=wnat[:].rearrange("m (u x) -> m u x", u=2),
-                in_=rows.rearrange("a b (u m e) k -> m (a b u) (e k)", u=2, e=2),
-            )
+            if plane == R_PLANE:
+                nc.sync.dma_start(
+                    out=wnat[:].rearrange("m (u x) -> m u x", u=2),
+                    in_=rows.rearrange("a b (u m e) k -> m (a b u) (e k)", u=2, e=2),
+                )
+            else:
+                nc.sync.dma_start(
+                    out=wnat[:].rearrange("m (t k) -> m t k", t=4),
+                    in_=rows.rearrange("a b (t m) k -> m (a b t) k", t=4),
+                )
             wn[plane] = wnat
 
         def load_h(queue, j):
-            size = SIZES[j]
             hnat = hpool.tile([P, 2048], BF16, name="hn", tag="hn")
             queue.dma_start(
-                out=hnat[:, 0 : 4 * size],
-                in_=hidden[starts[j] : starts[j] + size, :].rearrange("(p s) j -> p (s j)", s=size // P),
+                out=hnat[:].rearrange("p (s j) -> p s j", s=NSUB),
+                in_=hidden[j * N : (j + 1) * N, :].rearrange("(s p) j -> p s j", p=P),
             )
             hn[j] = hnat
 
@@ -87,31 +86,22 @@ def tile_grucell_t_kernel(
         load_w(G_PLANE, update_w_H2H)
         load_h(nc.sync, 2)
         nc.sync.dma_start(out=xb[:, X_FIRST:B], in_=xrow[X_FIRST:B].partition_broadcast(P))
-        for j in range(3, nblk):
+        for j in range(3, NBLK):
             load_h(nc.sync, j)
 
-        xp = const.tile([P, B], BF16, name="xp")
-        for j in range(nblk):
-            cols = slice(starts[j], starts[j] + SIZES[j])
-            nc.gpsimd.tensor_scalar(
-                out=xp[:, cols].rearrange("q (s p) -> q s p", s=SIZES[j] // P),
-                in0=xb[:, cols].rearrange("q (p s) -> q s p", s=SIZES[j] // P),
-                scalar1=1.0,
-                scalar2=0.0,
-                op0=ALU.mult,
-                op1=ALU.add,
-            )
+        negi = const.tile([P, P], BF16, name="negi")
+        nc.gpsimd.tensor_scalar(out=negi[:], in0=ident[:], scalar1=-1.0, scalar2=0.0, op0=ALU.mult, op1=ALU.add)
 
         wc = const.tile([P, 3 * 512], U32, name="wc", align_bytes=64)
         ws = const.tile([P, 3 * 512], U8, name="ws", align_bytes=64)
         gws = {}
 
-        def prep_w_tr(plane, engines, pool, tagname):
+        def prep_w_tr(plane, engines):
             words = wn[plane][:].bitcast(F32)
             gw = const.tile([P, 2048], BF16, name="gw%d" % plane, align_bytes=64)
             gww = gw[:].bitcast(F32)
             for u in range(2):
-                bank = pool.tile([P, 512], F32, name="tpw", tag=tagname)
+                bank = flp.tile([P, 512], F32, name="fl", tag="fl")
                 for e in range(2):
                     for kh in range(2):
                         nc.tensor.transpose(
@@ -134,302 +124,245 @@ def tile_grucell_t_kernel(
                 in_=gws[plane][:],
             )
 
-        identb = const.tile([P, P], BF16, name="identb")
-        make_identity(nc, identb[:])
-        prm = const.tile([P, 32], F32, name="prm")
-        nbz = const.tile([P, 4], F32, name="nbz")
-        prw = const.tile([P, 16], F32, name="prw")
+        prnf = const.tile([P, 256], F32, name="prnf")
+        prm = const.tile([P, 64], F32, name="prm")
 
         def prep_params():
-            bank = tp.tile([P, 512], F32, name="tpp", tag="tp")
-            nc.tensor.transpose(out=bank[:, 0:128], in_=prn[:].bitcast(F32), identity=ident[:])
-            nc.vector.tensor_copy(out=prw[:], in_=bank[:, 0:16])
-            nc.vector.tensor_copy(out=prm[:], in_=prw[:].bitcast(BF16))
-            nc.vector.tensor_scalar_mul(out=nbz[:], in0=prm[:, 8:12], scalar1=-1.0)
+            nc.vector.tensor_copy(out=prnf[:], in_=prn[:])
+            bank = flp.tile([P, 512], F32, name="fl", tag="fl")
+            views = [prnf[:, 0:128], prnf[:, 128:256], prnf[:, 0:256:2], prnf[:, 1:256:2]]
+            for j in range(4):
+                nc.tensor.transpose(out=bank[:, j * 128 : (j + 1) * 128], in_=views[j], identity=ident[:])
+            nc.vector.tensor_copy(
+                out=prm[:].rearrange("p (j r) -> p j r", j=4),
+                in_=bank[:].rearrange("p (j r) -> p j r", j=4)[:, :, 0:16],
+            )
 
-        W_COL = {Z_PLANE: 0, R_PLANE: 4, G_PLANE: 16}
-        B_COL = {Z_PLANE: 8, R_PLANE: 12, G_PLANE: 20}
+        def paired(row, t):
+            col = (2 + t % 2) * 16 + row + t // 2
+            return prm[:, col : col + 1]
 
-        hbank = {}
+        def natural(row, t):
+            col = (t % 2) * 16 + row + t // 2
+            return prm[:, col : col + 1]
+
         gh = {}
+        hbank = {}
         hcod = {}
-        banks_r = {}
-        banks_z = {}
+        banks = {}
         rr = {}
-        zz = {}
+        zc = {}
+        xw = {}
+        zbank = {}
+        uu = {}
         tt = {}
-        dq = {}
+        dbank = {}
         ghr = {}
         hrcod = {}
-        flb = {}
-        ot = {}
 
         def tr_h(j):
             words = hn[j][:].bitcast(F32)
-            nsub = SIZES[j] // P
             got = []
-            for first in range(0, nsub, 2):
-                subs = min(2, nsub - first)
-                bank = tp.tile([P, 512], F32, name="tph", tag="tp")
-                for sl in range(subs):
+            for first in range(0, NSUB, 2):
+                bank = flp.tile([P, 512], F32, name="fl", tag="fl")
+                for sl in range(2):
                     for u in range(2):
                         nc.tensor.transpose(
-                            out=bank[:, (u * subs + sl) * 128 : (u * subs + sl) * 128 + 128],
+                            out=bank[:, (u * 2 + sl) * 128 : (u * 2 + sl) * 128 + 128],
                             in_=words[:, (first + sl) * 256 + u * 128 : (first + sl) * 256 + u * 128 + 128],
                             identity=ident[:],
                         )
-                got.append((bank, first, subs))
+                got.append(bank)
             hbank[j] = got
 
         def ev_h(j):
-            g = p4.tile([P, 2048], BF16, name="gh", tag="gh", align_bytes=64)
+            g = p3.tile([P, 2048], BF16, name="gh", tag="gh", align_bytes=64)
             gwords = g[:].bitcast(F32)
-            for bank, first, subs in hbank[j]:
+            for half in range(2):
                 nc.scalar.copy(
-                    out=gwords[:, first * 256 : (first + subs) * 256].rearrange("p (n u) -> p n u", u=2),
-                    in_=bank[:, 0 : subs * 256].rearrange("p (u n) -> p n u", u=2),
+                    out=gwords[:, half * 512 : (half + 1) * 512].rearrange("p (n u) -> p n u", u=2),
+                    in_=hbank[j][half][:].rearrange("p (u n) -> p n u", u=2),
                 )
             gh[j] = g
 
-        def quantise(src, size, tagname):
+        def quantise(src, tagname):
             c = p2.tile([P, 512], U32, name=tagname + "c", tag=tagname + "c", align_bytes=64)
             s = p2.tile([P, 512], U8, name=tagname + "s", tag=tagname + "s", align_bytes=64)
-            nc.vector.quantize_mx(out=c[:, 0:size].bitcast(FP8X4), scales=s[:, 0:size], in_=src[:, 0 : 4 * size])
+            nc.vector.quantize_mx(out=c[:].bitcast(FP8X4), scales=s[:], in_=src[:])
             return (c, s)
 
-        def mx(plane, cs, size):
+        def mx(plane, cs):
             got = []
             for t in range(4):
                 bank = mxp.tile([P, 512], F32, name="mx", tag="mx")
                 col = plane * 512 + t * 128
                 nc.tensor.matmul_mx(
-                    out=bank[:, 0:size],
+                    out=bank[:],
                     lhsT=wc[:, col : col + 128].bitcast(FP8X4),
                     lhsT_scale=ws[:, col : col + 128],
-                    rhs=cs[0][:, 0:size].bitcast(FP8X4),
-                    rhs_scale=cs[1][:, 0:size],
+                    rhs=cs[0][:].bitcast(FP8X4),
+                    rhs_scale=cs[1][:],
                     start=True,
                     stop=True,
                 )
                 got.append(bank)
             return got
 
-        def gate(j, plane, banks, dst, func, q2):
-            size = SIZES[j]
-            nsub = size // P
-            xv = xp[:, starts[j] : starts[j] + size]
+        def gate(j, src, dst, func, wcol, bcol):
             for t in range(4):
-                seg = dst[:, t * size : (t + 1) * size]
+                seg = dst[:, t * N : (t + 1) * N]
                 nc.vector.scalar_tensor_tensor(
-                    out=seg,
-                    in0=xv,
-                    scalar=prm[:, W_COL[plane] + t : W_COL[plane] + t + 1],
-                    in1=banks[t][:, 0:size],
-                    op0=ALU.mult,
-                    op1=ALU.add,
+                    out=seg, in0=xb[:, j * N : (j + 1) * N], scalar=wcol(t), in1=src[t][:], op0=ALU.mult, op1=ALU.add
                 )
-                if plane == Z_PLANE:
-                    nc.scalar.activation(out=seg, in_=seg, func=func, bias=nbz[:, t : t + 1], scale=-1.0)
-                else:
-                    nc.scalar.activation(
-                        out=seg, in_=seg, func=func, bias=prm[:, B_COL[plane] + t : B_COL[plane] + t + 1], scale=1.0
-                    )
-                if t == 0 and q2 is not None:
-                    hrcod[q2] = quantise(ghr[q2], SIZES[q2], "r")
-
-        def diff(eng, j, t0, t1):
-            size = SIZES[j]
-            eng.tensor_tensor(
-                out=dq[j][:, t0 * size : t1 * size].rearrange("p (t n) -> p t n", t=t1 - t0),
-                in0=tt[j][:, t0 * size : t1 * size].rearrange("p (t n) -> p t n", t=t1 - t0),
-                in1=gh[j][:, 0 : 4 * size].rearrange("p (n t) -> p t n", t=4)[:, t0:t1, :],
-                op=ALU.subtract,
-            )
-
-        def prod(eng, j, t0, t1):
-            size = SIZES[j]
-            cols = slice(t0 * size, t1 * size)
-            eng.tensor_tensor(out=dq[j][:, cols], in0=zz[j][:, cols], in1=dq[j][:, cols], op=ALU.mult)
-
-        def flip(j, s):
-            size = SIZES[j]
-            bank = flp.tile([P, 512], F32, name="fl", tag="fl")
-            nc.tensor.matmul(
-                out=bank[:],
-                lhsT=identb[:],
-                rhs=hn[j][:, s * 512 : (s + 1) * 512].rearrange("b (u p e) -> b u e p", u=2, e=2),
-                start=True,
-                stop=False,
-            )
-            for t in range(4):
-                lo = t * size + s * 128
-                nc.tensor.matmul(
-                    out=bank[:, t * 128 : (t + 1) * 128],
-                    lhsT=dq[j][:, lo : lo + 128],
-                    rhs=ident[:],
-                    is_transpose=True,
-                    start=False,
-                    stop=(t == 3),
-                )
-            flb[(j, s)] = bank
-
-        def ev_out(j, s):
-            nc.scalar.copy(
-                out=ot[j][:, s * 512 : (s + 1) * 512].rearrange("b (u p e) -> b u p e", u=2, e=2),
-                in_=flb[(j, s)][:].rearrange("b (u e p) -> b u p e", u=2, e=2),
-            )
-
-        def finish_a(j):
-            flip(j, 0)
-            flip(j, 1)
-
-        def finish_b(j):
-            size = SIZES[j]
-            nsub = size // P
-            otile = p2.tile([P, 2048], F32, name="ot", tag="ot")
-            ot[j] = otile
-            for s in range(2, nsub):
-                ev_out(j, s - 2)
-                flip(j, s)
-            ev_out(j, nsub - 2)
-            ev_out(j, nsub - 1)
-            nc.sync.dma_start(
-                out=out[starts[j] : starts[j] + size, :].rearrange("(p s) c -> p (s c)", s=nsub),
-                in_=otile[:, 0 : nsub * 512],
-            )
-
-        def ok(j):
-            return 0 <= j < nblk
-
-        def rows_view(tile_ap, j, s):
-            size = SIZES[j]
-            return tile_ap[:, 0 : 4 * size].rearrange("p (t n) -> p t n", t=4)[:, :, s * 128 : (s + 1) * 128]
-
-        def diff_rows(j, s):
-            size = SIZES[j]
-            nc.vector.tensor_tensor(
-                out=rows_view(dq[j], j, s),
-                in0=rows_view(tt[j], j, s),
-                in1=gh[j][:, 0 : 4 * size].rearrange("p (n t) -> p t n", t=4)[:, :, s * 128 : (s + 1) * 128],
-                op=ALU.subtract,
-            )
-
-        def prod_rows(j, s):
-            nc.vector.tensor_tensor(
-                out=rows_view(dq[j], j, s), in0=rows_view(zz[j], j, s), in1=rows_view(dq[j], j, s), op=ALU.mult
-            )
-
-        def finish_rows(j, s):
-            size = SIZES[j]
-            flip(j, s)
-            ev_out(j, s)
-            nc.sync.dma_start(
-                out=out[starts[j] : starts[j] + size, :].rearrange("(p s) c -> p s c", s=size // P)[:, s, :],
-                in_=ot[j][:, s * 512 : (s + 1) * 512],
-            )
-
-        last = nblk - 1
-        banks_g = {}
-
-        def g_share(j):
-            return G_Q_T if j < last - 1 else 2
+                nc.scalar.activation(out=seg, in_=seg, func=func, bias=bcol(t), scale=1.0)
 
         def gates_r(i):
             rtile = p2.tile([P, 2048], F32, name="rr", tag="rr")
             rr[i] = rtile
-            gate(i, R_PLANE, banks_r[i], rtile, ACT.Sigmoid, None)
+            gate(i, banks["r", i], rtile, ACT.Sigmoid, lambda t: paired(2, t), lambda t: paired(6, t))
 
         def gates_g(j):
             ttile = p2.tile([P, 2048], F32, name="tt", tag="tt")
             tt[j] = ttile
-            gate(j, G_PLANE, banks_g[j], ttile, ACT.Tanh, None)
-            dtile = p2.tile([P, 2048], F32, name="dq", tag="dq")
-            dq[j] = dtile
-            if j != last:
-                for t in (3, 2, 1, 0):
-                    diff(nc.gpsimd, j, t, t + 1)
-                for t in range(g_share(j)):
-                    prod(nc.gpsimd, j, t, t + 1)
+            gate(j, banks["g", j], ttile, ACT.Tanh, lambda t: natural(8, t), lambda t: natural(10, t))
 
-        def gates_z(i):
-            ztile = p3.tile([P, 2048], F32, name="zz", tag="zz")
-            zz[i] = ztile
-            gate(i, Z_PLANE, banks_z[i], ztile, ACT.Sigmoid, i)
+        def x_term(j):
+            w = p2.tile([P, 2048], F32, name="xw", tag="xw")
+            for t in range(4):
+                nc.gpsimd.tensor_scalar(
+                    out=w[:, t * N : (t + 1) * N],
+                    in0=xb[:, j * N : (j + 1) * N],
+                    scalar1=natural(0, t),
+                    scalar2=natural(4, t),
+                    op0=ALU.mult,
+                    op1=ALU.add,
+                )
+            xw[j] = w
+
+        def copy_z(j):
+            c = p2.tile([P, 2048], F32, name="zc", tag="zc")
+            for t in range(4):
+                nc.scalar.copy(out=c[:, t * N : (t + 1) * N], in_=banks["z", j][t][:])
+            zc[j] = c
+
+        def flip_z(j):
+            got = []
+            for s in range(NSUB):
+                bank = flp.tile([P, 512], F32, name="fl", tag="fl")
+                for t in range(4):
+                    lo = t * N + s * P
+                    for k, src in enumerate((zc[j], xw[j])):
+                        nc.tensor.matmul(
+                            out=bank[:, t * P : (t + 1) * P],
+                            lhsT=src[:, lo : lo + P],
+                            rhs=ident[:],
+                            is_transpose=True,
+                            start=(k == 0),
+                            stop=(k == 1),
+                        )
+                got.append(bank)
+            zbank[j] = got
+
+        def act_z(j):
+            u = p2.tile([P, 2048], F32, name="uu", tag="uu")
+            for s in range(NSUB):
+                nc.scalar.activation(
+                    out=u[:, s * D : (s + 1) * D], in_=zbank[j][s][:], func=ACT.Sigmoid, bias=0.0, scale=-1.0
+                )
+            uu[j] = u
+
+        def flip_t(j):
+            got = []
+            for s in range(NSUB):
+                bank = flp.tile([P, 512], F32, name="fl", tag="fl")
+                nc.tensor.matmul(
+                    out=bank[:], lhsT=negi[:], rhs=hn[j][:, s * D : (s + 1) * D], start=True, stop=False
+                )
+                for t in range(4):
+                    lo = t * N + s * P
+                    nc.tensor.matmul(
+                        out=bank[:, t * P : (t + 1) * P],
+                        lhsT=tt[j][:, lo : lo + P],
+                        rhs=ident[:],
+                        is_transpose=True,
+                        start=False,
+                        stop=(t == 3),
+                    )
+                got.append(bank)
+            dbank[j] = got
+
+        def blend(j, adder, pieces):
+            o = p3.tile([P, 2048], F32, name="ot", tag="ot")
+            rows = out[j * N : (j + 1) * N, :].rearrange("(s p) c -> p s c", p=P)
+            per = NSUB // pieces
+            for s in range(NSUB):
+                cols = slice(s * D, (s + 1) * D)
+                nc.vector.tensor_tensor(out=o[:, cols], in0=uu[j][:, cols], in1=dbank[j][s][:], op=ALU.mult)
+                adder.tensor_tensor(out=o[:, cols], in0=o[:, cols], in1=hn[j][:, cols], op=ALU.add)
+                if (s + 1) % per == 0:
+                    lo = s + 1 - per
+                    nc.sync.dma_start(
+                        out=rows[:, lo : s + 1, :],
+                        in_=o[:, lo * D : (s + 1) * D].rearrange("p (s c) -> p s c", s=per),
+                    )
 
         def h_times_r(i):
             hrt = p2.tile([P, 2048], BF16, name="ghr", tag="ghr", align_bytes=64)
             ghr[i] = hrt
-            size = SIZES[i]
-            for bank, first, subs in hbank[i]:
+            for half in range(2):
+                words = slice(half * 1024, (half + 1) * 1024)
                 nc.vector.tensor_tensor(
-                    out=hrt[:, first * 512 : (first + subs) * 512].rearrange("p (n u e) -> p n u e", u=2, e=2),
-                    in0=rr[i][:, 0 : 4 * size].rearrange("p (u e n) -> p n u e", u=2, e=2)[
-                        :, first * 128 : (first + subs) * 128, :, :
-                    ],
-                    in1=bank[:, 0 : subs * 256].bitcast(BF16).rearrange("p (u n e) -> p n u e", u=2, e=2),
+                    out=hrt[:, words].rearrange("p (c i t) -> p c t i", i=4, t=4),
+                    in0=rr[i][:].rearrange("p (t c i) -> p c t i", t=4, i=4)[:, half * 64 : (half + 1) * 64, :, :],
+                    in1=gh[i][:, words].rearrange("p (c i t) -> p c t i", i=4, t=4),
                     op=ALU.mult,
                 )
 
-        def last_block():
-            nsub = SIZES[last] // P
-            otile = p2.tile([P, 2048], F32, name="ot", tag="ot")
-            ot[last] = otile
-            diff_rows(last, 0)
-            for s in range(nsub):
-                if s + 1 < nsub:
-                    diff_rows(last, s + 1)
-                prod_rows(last, s)
-                finish_rows(last, s)
-
-        prep_w_tr(R_PLANE, "vs", tp, "tp")
+        prep_w_tr(R_PLANE, "vs")
         tr_h(0)
         ev_h(0)
         prep_w_q(R_PLANE)
         prep_params()
-        prep_w_tr(Z_PLANE, "ss", flp, "fl")
-        hcod[0] = quantise(gh[0], SIZES[0], "h")
-        banks_r[0] = mx(R_PLANE, hcod[0], SIZES[0])
+        prep_w_tr(Z_PLANE, "ss")
+        hcod[0] = quantise(gh[0], "h")
+        banks["r", 0] = mx(R_PLANE, hcod[0])
+        x_term(0)
 
-        gates_r(0)
-        prep_w_q(Z_PLANE)
-        tr_h(0)
-        prep_w_tr(G_PLANE, "ss", flp, "fl")
-        banks_z[0] = mx(Z_PLANE, hcod[0], SIZES[0])
-        h_times_r(0)
-        tr_h(1)
-        ev_h(1)
-        gates_z(0)
-        hcod[1] = quantise(gh[1], SIZES[1], "h")
-        prep_w_q(G_PLANE)
-        banks_r[1] = mx(R_PLANE, hcod[1], SIZES[1])
-        tr_h(2)
-        ev_h(2)
-
-        for i in range(1, nblk):
+        for i in range(NBLK):
             gates_r(i)
-            banks_g[i - 1] = mx(G_PLANE, hrcod[i - 1], SIZES[i - 1])
-            if i >= 2:
-                prod(nc.vector, i - 2, g_share(i - 2), 4)
-            tr_h(i)
-            if i >= 2:
-                finish_a(i - 2)
-            gates_g(i - 1)
-            banks_z[i] = mx(Z_PLANE, hcod[i], SIZES[i])
-            if i >= 2:
-                finish_b(i - 2)
-            if i + 1 < nblk:
-                hcod[i + 1] = quantise(gh[i + 1], SIZES[i + 1], "h")
+            if i == 0:
+                prep_w_q(Z_PLANE)
+            if i + 1 < NBLK:
+                tr_h(i + 1)
+                ev_h(i + 1)
+            if i > 0:
+                banks["g", i - 1] = mx(G_PLANE, hrcod[i - 1])
+                flip_z(i - 1)
+                gates_g(i - 1)
+            else:
+                prep_w_tr(G_PLANE, "ss")
+            banks["z", i] = mx(Z_PLANE, hcod[i])
+            if i > 0:
+                act_z(i - 1)
             h_times_r(i)
-            if i + 2 < nblk:
-                tr_h(i + 2)
-                ev_h(i + 2)
-            gates_z(i)
-            if i + 1 < nblk:
-                banks_r[i + 1] = mx(R_PLANE, hcod[i + 1], SIZES[i + 1])
+            if i + 1 < NBLK:
+                hcod[i + 1] = quantise(gh[i + 1], "h")
+            hrcod[i] = quantise(ghr[i], "r")
+            if i == 0:
+                prep_w_q(G_PLANE)
+            if i > 0:
+                flip_t(i - 1)
+            copy_z(i)
+            if i + 1 < NBLK:
+                banks["r", i + 1] = mx(R_PLANE, hcod[i + 1])
+            if i > 0:
+                blend(i - 1, nc.gpsimd, 2)
+            if i + 1 < NBLK:
+                x_term(i + 1)
 
-        banks_g[last] = mx(G_PLANE, hrcod[last], SIZES[last])
-        gates_g(last)
-        prod(nc.vector, last - 1, g_share(last - 1), 4)
-        finish_a(last - 1)
-        finish_b(last - 1)
-        last_block()
+        banks["g", LAST] = mx(G_PLANE, hrcod[LAST])
+        flip_z(LAST)
+        act_z(LAST)
+        gates_g(LAST)
+        flip_t(LAST)
+        blend(LAST, nc.vector, 4)

@@ -14,16 +14,17 @@ ACT = mybir.ActivationFunctionType
 P = 128
 B = 4096
 D = 512
-N = 512
-NSUB = N // P
-NBLK = B // N
+SIZES = [256, 512, 512, 512, 512, 512, 512, 512, 256]
+NBLK = len(SIZES)
+STARTS = [sum(SIZES[:j]) for j in range(NBLK)]
 LAST = NBLK - 1
 FLOPS = 2 * B * D * 3 * D
 
 R_PLANE = 0
 Z_PLANE = 1
 G_PLANE = 2
-X_FIRST = 2 * N
+X_FIRST = SIZES[0]
+assert sum(SIZES) == B
 
 
 def tile_grucell_t_kernel(
@@ -41,11 +42,10 @@ def tile_grucell_t_kernel(
 
         ident = const.tile([P, P], F32, name="ident")
         make_identity(nc, ident[:])
-        warm = const.tile([P, 1], F32, name="warm")
-        nc.vector.memset(warm[:], 0.0)
-        nc.scalar.activation(out=warm[:], in_=warm[:], func=ACT.Sigmoid)
         prn = const.tile([P, 256], BF16, name="prn")
         nc.vector.memset(prn[:], 0.0)
+        warm = const.tile([P, 1], F32, name="warm")
+        nc.vector.memset(warm[:], 0.0)
 
         wn = {}
         hn = {}
@@ -67,26 +67,26 @@ def tile_grucell_t_kernel(
         def load_h(queue, j):
             hnat = hpool.tile([P, 2048], BF16, name="hn", tag="hn")
             queue.dma_start(
-                out=hnat[:].rearrange("p (s j) -> p s j", s=NSUB),
-                in_=hidden[j * N : (j + 1) * N, :].rearrange("(s p) j -> p s j", p=P),
+                out=hnat[:, 0 : 4 * SIZES[j]].rearrange("p (s j) -> p s j", j=D),
+                in_=hidden[STARTS[j] : STARTS[j] + SIZES[j], :].rearrange("(s p) j -> p s j", p=P),
             )
             hn[j] = hnat
 
         xb = const.tile([P, B], BF16, name="xb")
         xrow = inputs.rearrange("b o -> (b o)")
-        load_w(R_PLANE, gate_w_H2H[:, :, D : 2 * D, :])
-        load_h(nc.scalar, 0)
         nc.scalar.dma_start(out=prn[0:4, :], in_=gate_w_I2H.rearrange("a b (r k) c -> (a b r) (k c)", k=256))
         nc.scalar.dma_start(out=prn[4:8, :], in_=gate_bias.rearrange("(r k) -> r k", k=256))
         nc.scalar.dma_start(out=prn[8:10, :], in_=update_w_I2H.rearrange("a b (r k) c -> (a b r) (k c)", k=256))
         nc.scalar.dma_start(out=prn[10:12, :], in_=update_bias.rearrange("(r k) -> r k", k=256))
-        nc.scalar.dma_start(out=xb[:, 0:X_FIRST], in_=xrow[0:X_FIRST].partition_broadcast(P))
+        nc.scalar.activation(out=warm[:], in_=warm[:], func=ACT.Sigmoid)
+        load_w(R_PLANE, gate_w_H2H[:, :, D : 2 * D, :])
+        load_h(nc.sync, 0)
+        nc.sync.dma_start(out=xb[:, 0:X_FIRST], in_=xrow[0:X_FIRST].partition_broadcast(P))
         load_w(Z_PLANE, gate_w_H2H[:, :, 0:D, :])
         load_h(nc.sync, 1)
         load_w(G_PLANE, update_w_H2H)
-        load_h(nc.sync, 2)
         nc.sync.dma_start(out=xb[:, X_FIRST:B], in_=xrow[X_FIRST:B].partition_broadcast(P))
-        for j in range(3, NBLK):
+        for j in range(2, NBLK):
             load_h(nc.sync, j)
 
         negi = const.tile([P, P], BF16, name="negi")
@@ -163,7 +163,7 @@ def tile_grucell_t_kernel(
         def tr_h(j):
             words = hn[j][:].bitcast(F32)
             got = []
-            for first in range(0, NSUB, 2):
+            for first in range(0, SIZES[j] // P, 2):
                 bank = flp.tile([P, 512], F32, name="fl", tag="fl")
                 for sl in range(2):
                     for u in range(2):
@@ -178,41 +178,45 @@ def tile_grucell_t_kernel(
         def ev_h(j):
             g = p3.tile([P, 2048], BF16, name="gh", tag="gh", align_bytes=64)
             gwords = g[:].bitcast(F32)
-            for half in range(2):
+            for k, bank in enumerate(hbank[j]):
                 nc.scalar.copy(
-                    out=gwords[:, half * 512 : (half + 1) * 512].rearrange("p (n u) -> p n u", u=2),
-                    in_=hbank[j][half][:].rearrange("p (u n) -> p n u", u=2),
+                    out=gwords[:, k * 512 : (k + 1) * 512].rearrange("p (n u) -> p n u", u=2),
+                    in_=bank[:].rearrange("p (u n) -> p n u", u=2),
                 )
             gh[j] = g
 
-        def quantise(src, tagname):
+        def quantise(src, n, tagname):
             c = p2.tile([P, 512], U32, name=tagname + "c", tag=tagname + "c", align_bytes=64)
             s = p2.tile([P, 512], U8, name=tagname + "s", tag=tagname + "s", align_bytes=64)
-            nc.vector.quantize_mx(out=c[:].bitcast(FP8X4), scales=s[:], in_=src[:])
+            nc.vector.quantize_mx(out=c[:, 0:n].bitcast(FP8X4), scales=s[:, 0:n], in_=src[:, 0 : 4 * n])
             return (c, s)
 
-        def mx(plane, cs):
+        def mx(plane, cs, n):
             got = []
             for t in range(4):
                 bank = mxp.tile([P, 512], F32, name="mx", tag="mx")
                 col = plane * 512 + t * 128
                 nc.tensor.matmul_mx(
-                    out=bank[:],
+                    out=bank[:, 0:n],
                     lhsT=wc[:, col : col + 128].bitcast(FP8X4),
                     lhsT_scale=ws[:, col : col + 128],
-                    rhs=cs[0][:].bitcast(FP8X4),
-                    rhs_scale=cs[1][:],
+                    rhs=cs[0][:, 0:n].bitcast(FP8X4),
+                    rhs_scale=cs[1][:, 0:n],
                     start=True,
                     stop=True,
                 )
                 got.append(bank)
             return got
 
+        def xrow_of(j):
+            return xb[:, STARTS[j] : STARTS[j] + SIZES[j]]
+
         def gate(j, src, dst, func, wcol, bcol):
+            n = SIZES[j]
             for t in range(4):
-                seg = dst[:, t * N : (t + 1) * N]
+                seg = dst[:, t * n : (t + 1) * n]
                 nc.vector.scalar_tensor_tensor(
-                    out=seg, in0=xb[:, j * N : (j + 1) * N], scalar=wcol(t), in1=src[t][:], op0=ALU.mult, op1=ALU.add
+                    out=seg, in0=xrow_of(j), scalar=wcol(t), in1=src[t][:, 0:n], op0=ALU.mult, op1=ALU.add
                 )
                 nc.scalar.activation(out=seg, in_=seg, func=func, bias=bcol(t), scale=1.0)
 
@@ -228,10 +232,11 @@ def tile_grucell_t_kernel(
 
         def x_term(j):
             w = p2.tile([P, 2048], F32, name="xw", tag="xw")
+            n = SIZES[j]
             for t in range(4):
                 nc.gpsimd.tensor_scalar(
-                    out=w[:, t * N : (t + 1) * N],
-                    in0=xb[:, j * N : (j + 1) * N],
+                    out=w[:, t * n : (t + 1) * n],
+                    in0=xrow_of(j),
                     scalar1=natural(0, t),
                     scalar2=natural(4, t),
                     op0=ALU.mult,
@@ -241,16 +246,17 @@ def tile_grucell_t_kernel(
 
         def copy_z(j):
             c = p2.tile([P, 2048], F32, name="zc", tag="zc")
+            n = SIZES[j]
             for t in range(4):
-                nc.scalar.copy(out=c[:, t * N : (t + 1) * N], in_=banks["z", j][t][:])
+                nc.scalar.copy(out=c[:, t * n : (t + 1) * n], in_=banks["z", j][t][:, 0:n])
             zc[j] = c
 
         def flip_z(j):
             got = []
-            for s in range(NSUB):
+            for s in range(SIZES[j] // P):
                 bank = flp.tile([P, 512], F32, name="fl", tag="fl")
                 for t in range(4):
-                    lo = t * N + s * P
+                    lo = t * SIZES[j] + s * P
                     for k, src in enumerate((zc[j], xw[j])):
                         nc.tensor.matmul(
                             out=bank[:, t * P : (t + 1) * P],
@@ -265,7 +271,7 @@ def tile_grucell_t_kernel(
 
         def act_z(j):
             u = p2.tile([P, 2048], F32, name="uu", tag="uu")
-            for s in range(NSUB):
+            for s in range(SIZES[j] // P):
                 nc.scalar.activation(
                     out=u[:, s * D : (s + 1) * D], in_=zbank[j][s][:], func=ACT.Sigmoid, bias=0.0, scale=-1.0
                 )
@@ -273,13 +279,13 @@ def tile_grucell_t_kernel(
 
         def flip_t(j):
             got = []
-            for s in range(NSUB):
+            for s in range(SIZES[j] // P):
                 bank = flp.tile([P, 512], F32, name="fl", tag="fl")
                 nc.tensor.matmul(
                     out=bank[:], lhsT=negi[:], rhs=hn[j][:, s * D : (s + 1) * D], start=True, stop=False
                 )
                 for t in range(4):
-                    lo = t * N + s * P
+                    lo = t * SIZES[j] + s * P
                     nc.tensor.matmul(
                         out=bank[:, t * P : (t + 1) * P],
                         lhsT=tt[j][:, lo : lo + P],
@@ -291,11 +297,10 @@ def tile_grucell_t_kernel(
                 got.append(bank)
             dbank[j] = got
 
-        def blend(j, adder, pieces):
+        def blend(j, adder, per):
             o = p3.tile([P, 2048], F32, name="ot", tag="ot")
-            rows = out[j * N : (j + 1) * N, :].rearrange("(s p) c -> p s c", p=P)
-            per = NSUB // pieces
-            for s in range(NSUB):
+            rows = out[STARTS[j] : STARTS[j] + SIZES[j], :].rearrange("(s p) c -> p s c", p=P)
+            for s in range(SIZES[j] // P):
                 cols = slice(s * D, (s + 1) * D)
                 nc.vector.tensor_tensor(out=o[:, cols], in0=uu[j][:, cols], in1=dbank[j][s][:], op=ALU.mult)
                 adder.tensor_tensor(out=o[:, cols], in0=o[:, cols], in1=hn[j][:, cols], op=ALU.add)
@@ -306,14 +311,28 @@ def tile_grucell_t_kernel(
                         in_=o[:, lo * D : (s + 1) * D].rearrange("p (s c) -> p s c", s=per),
                     )
 
+        def blend_last(j):
+            nsub = SIZES[j] // P
+            o = p3.tile([P, 2048], F32, name="ot", tag="ot")
+            rows = out[STARTS[j] : STARTS[j] + SIZES[j], :].rearrange("(s p) c -> p s c", p=P)
+            for s in range(nsub):
+                cols = slice(s * D, (s + 1) * D)
+                nc.vector.tensor_tensor(out=o[:, cols], in0=uu[j][:, cols], in1=dbank[j][s][:], op=ALU.mult)
+            for s in range(nsub):
+                cols = slice(s * D, (s + 1) * D)
+                nc.vector.tensor_tensor(out=o[:, cols], in0=o[:, cols], in1=hn[j][:, cols], op=ALU.add)
+                nc.sync.dma_start(out=rows[:, s, :], in_=o[:, cols])
+
         def h_times_r(i):
             hrt = p2.tile([P, 2048], BF16, name="ghr", tag="ghr", align_bytes=64)
             ghr[i] = hrt
-            for half in range(2):
+            for half in range(SIZES[i] // 256):
                 words = slice(half * 1024, (half + 1) * 1024)
                 nc.vector.tensor_tensor(
                     out=hrt[:, words].rearrange("p (c i t) -> p c t i", i=4, t=4),
-                    in0=rr[i][:].rearrange("p (t c i) -> p c t i", t=4, i=4)[:, half * 64 : (half + 1) * 64, :, :],
+                    in0=rr[i][:, 0 : 4 * SIZES[i]].rearrange("p (t c i) -> p c t i", t=4, i=4)[
+                        :, half * 64 : (half + 1) * 64, :, :
+                    ],
                     in1=gh[i][:, words].rearrange("p (c i t) -> p c t i", i=4, t=4),
                     op=ALU.mult,
                 )
@@ -324,8 +343,8 @@ def tile_grucell_t_kernel(
         prep_w_q(R_PLANE)
         prep_params()
         prep_w_tr(Z_PLANE, "ss")
-        hcod[0] = quantise(gh[0], "h")
-        banks["r", 0] = mx(R_PLANE, hcod[0])
+        hcod[0] = quantise(gh[0], SIZES[0], "h")
+        banks["r", 0] = mx(R_PLANE, hcod[0], SIZES[0])
         x_term(0)
 
         for i in range(NBLK):
@@ -336,33 +355,33 @@ def tile_grucell_t_kernel(
                 tr_h(i + 1)
                 ev_h(i + 1)
             if i > 0:
-                banks["g", i - 1] = mx(G_PLANE, hrcod[i - 1])
+                banks["g", i - 1] = mx(G_PLANE, hrcod[i - 1], SIZES[i - 1])
                 flip_z(i - 1)
                 gates_g(i - 1)
             else:
                 prep_w_tr(G_PLANE, "ss")
-            banks["z", i] = mx(Z_PLANE, hcod[i])
+            banks["z", i] = mx(Z_PLANE, hcod[i], SIZES[i])
             if i > 0:
                 act_z(i - 1)
             h_times_r(i)
             if i + 1 < NBLK:
-                hcod[i + 1] = quantise(gh[i + 1], "h")
-            hrcod[i] = quantise(ghr[i], "r")
+                hcod[i + 1] = quantise(gh[i + 1], SIZES[i + 1], "h")
+            hrcod[i] = quantise(ghr[i], SIZES[i], "r")
             if i == 0:
                 prep_w_q(G_PLANE)
             if i > 0:
                 flip_t(i - 1)
             copy_z(i)
             if i + 1 < NBLK:
-                banks["r", i + 1] = mx(R_PLANE, hcod[i + 1])
+                banks["r", i + 1] = mx(R_PLANE, hcod[i + 1], SIZES[i + 1])
             if i > 0:
                 blend(i - 1, nc.gpsimd, 2)
             if i + 1 < NBLK:
                 x_term(i + 1)
 
-        banks["g", LAST] = mx(G_PLANE, hrcod[LAST])
+        banks["g", LAST] = mx(G_PLANE, hrcod[LAST], SIZES[LAST])
         flip_z(LAST)
         act_z(LAST)
         gates_g(LAST)
         flip_t(LAST)
-        blend(LAST, nc.vector, 4)
+        blend_last(LAST)

@@ -53,10 +53,11 @@ def tile_grucell_t_kernel(
         def load_w(plane, rows):
             wnat = const.tile([P, 2048], BF16, name="wn%d" % plane)
             if plane == R_PLANE:
-                nc.sync.dma_start(
-                    out=wnat[:].rearrange("m (u x) -> m u x", u=2),
-                    in_=rows.rearrange("a b (u m e) k -> m (a b u) (e k)", u=2, e=2),
-                )
+                for u in range(2):
+                    nc.sync.dma_start(
+                        out=wnat[:, u * 1024 : (u + 1) * 1024],
+                        in_=rows[:, :, u * 256 : (u + 1) * 256, :].rearrange("a b (m e) k -> m (a b e k)", e=2),
+                    )
             else:
                 nc.sync.dma_start(
                     out=wnat[:].rearrange("m (t k) -> m t k", t=4),
@@ -127,8 +128,10 @@ def tile_grucell_t_kernel(
         prnf = const.tile([P, 256], F32, name="prnf")
         prm = const.tile([P, 64], F32, name="prm")
 
-        def prep_params():
+        def prep_params_in():
             nc.vector.tensor_copy(out=prnf[:], in_=prn[:])
+
+        def prep_params():
             bank = flp.tile([P, 512], F32, name="fl", tag="fl")
             views = [prnf[:, 0:128], prnf[:, 128:256], prnf[:, 0:256:2], prnf[:, 1:256:2]]
             for j in range(4):
@@ -157,6 +160,7 @@ def tile_grucell_t_kernel(
         uu = {}
         tt = {}
         dbank = {}
+        ot = {}
         ghr = {}
         hrcod = {}
 
@@ -297,10 +301,13 @@ def tile_grucell_t_kernel(
                 got.append(bank)
             dbank[j] = got
 
-        def blend(j, adder, per):
-            o = p3.tile([P, 2048], F32, name="ot", tag="ot")
+        def blend(j, adder, per, first, end):
+            if first == 0:
+                o = p3.tile([P, 2048], F32, name="ot", tag="ot")
+                ot[j] = o
+            o = ot[j]
             rows = out[STARTS[j] : STARTS[j] + SIZES[j], :].rearrange("(s p) c -> p s c", p=P)
-            for s in range(SIZES[j] // P):
+            for s in range(first, end):
                 cols = slice(s * D, (s + 1) * D)
                 nc.vector.tensor_tensor(out=o[:, cols], in0=uu[j][:, cols], in1=dbank[j][s][:], op=ALU.mult)
                 adder.tensor_tensor(out=o[:, cols], in0=o[:, cols], in1=hn[j][:, cols], op=ALU.add)
@@ -326,24 +333,22 @@ def tile_grucell_t_kernel(
         def h_times_r(i):
             hrt = p2.tile([P, 2048], BF16, name="ghr", tag="ghr", align_bytes=64)
             ghr[i] = hrt
-            for half in range(SIZES[i] // 256):
-                words = slice(half * 1024, (half + 1) * 1024)
-                nc.vector.tensor_tensor(
-                    out=hrt[:, words].rearrange("p (c i t) -> p c t i", i=4, t=4),
-                    in0=rr[i][:, 0 : 4 * SIZES[i]].rearrange("p (t c i) -> p c t i", t=4, i=4)[
-                        :, half * 64 : (half + 1) * 64, :, :
-                    ],
-                    in1=gh[i][:, words].rearrange("p (c i t) -> p c t i", i=4, t=4),
-                    op=ALU.mult,
-                )
+            words = slice(0, 4 * SIZES[i])
+            nc.vector.tensor_tensor(
+                out=hrt[:, words].rearrange("p (c i t) -> p c t i", i=4, t=4),
+                in0=rr[i][:, words].rearrange("p (t c i) -> p c t i", t=4, i=4),
+                in1=gh[i][:, words].rearrange("p (c i t) -> p c t i", i=4, t=4),
+                op=ALU.mult,
+            )
 
         prep_w_tr(R_PLANE, "vs")
+        prep_params_in()
         tr_h(0)
         ev_h(0)
         prep_w_q(R_PLANE)
+        hcod[0] = quantise(gh[0], SIZES[0], "h")
         prep_params()
         prep_w_tr(Z_PLANE, "ss")
-        hcod[0] = quantise(gh[0], SIZES[0], "h")
         banks["r", 0] = mx(R_PLANE, hcod[0], SIZES[0])
         x_term(0)
 
@@ -375,13 +380,15 @@ def tile_grucell_t_kernel(
             if i + 1 < NBLK:
                 banks["r", i + 1] = mx(R_PLANE, hcod[i + 1], SIZES[i + 1])
             if i > 0:
-                blend(i - 1, nc.gpsimd, 2)
+                nsub = SIZES[i - 1] // P
+                blend(i - 1, nc.gpsimd, 2, 0, nsub if i < LAST else nsub // 2)
             if i + 1 < NBLK:
                 x_term(i + 1)
 
         banks["g", LAST] = mx(G_PLANE, hrcod[LAST], SIZES[LAST])
         flip_z(LAST)
-        act_z(LAST)
         gates_g(LAST)
+        blend(LAST - 1, nc.gpsimd, 1, SIZES[LAST - 1] // P // 2, SIZES[LAST - 1] // P)
+        act_z(LAST)
         flip_t(LAST)
         blend_last(LAST)

@@ -24,6 +24,10 @@ R_PLANE = 0
 Z_PLANE = 1
 G_PLANE = 2
 X_FIRST = SIZES[0]
+X_GROUPS = [[0], [1, 2], [3, 4], [5, 6], [7, 8]]
+XG_START = [STARTS[g[0]] for g in X_GROUPS]
+XG_SIZE = [sum([SIZES[j] for j in g]) for g in X_GROUPS]
+X_PLAN = {0: 5, 1: 2, 2: 2, 3: 2, 4: 2, 5: 2, 6: 1}
 assert sum(SIZES) == B
 
 
@@ -34,6 +38,7 @@ def tile_grucell_t_kernel(
     with ExitStack() as ctx:
         const = ctx.enter_context(tc.tile_pool(name="const", bufs=1))
         hpool = ctx.enter_context(tc.tile_pool(name="hpool", bufs=NBLK))
+        p1 = ctx.enter_context(tc.tile_pool(name="p1", bufs=1))
         p2 = ctx.enter_context(tc.tile_pool(name="p2", bufs=2))
         p3 = ctx.enter_context(tc.tile_pool(name="p3", bufs=3))
         mxp = ctx.enter_context(tc.psum_pool(name="mxp", bufs=4))
@@ -225,31 +230,31 @@ def tile_grucell_t_kernel(
                 nc.scalar.activation(out=seg, in_=seg, func=func, bias=bcol(t), scale=1.0)
 
         def gates_r(i):
-            rtile = p2.tile([P, 2048], F32, name="rr", tag="rr")
+            rtile = p1.tile([P, 2048], F32, name="rr", tag="rr")
             rr[i] = rtile
             gate(i, banks["r", i], rtile, ACT.Sigmoid, lambda t: paired(2, t), lambda t: paired(6, t))
 
         def gates_g(j):
-            ttile = p2.tile([P, 2048], F32, name="tt", tag="tt")
+            ttile = p1.tile([P, 2048], F32, name="tt", tag="tt")
             tt[j] = ttile
             gate(j, banks["g", j], ttile, ACT.Tanh, lambda t: natural(8, t), lambda t: natural(10, t))
 
-        def x_term(j):
-            w = p2.tile([P, 2048], F32, name="xw", tag="xw")
-            n = SIZES[j]
-            for t in range(4):
-                nc.gpsimd.tensor_scalar(
-                    out=w[:, t * n : (t + 1) * n],
-                    in0=xrow_of(j),
-                    scalar1=natural(0, t),
-                    scalar2=natural(4, t),
-                    op0=ALU.mult,
-                    op1=ALU.add,
-                )
-            xw[j] = w
+        def x_term(g, t):
+            lo, n = XG_START[g], XG_SIZE[g]
+            if t == 0:
+                w = const.tile([P, 4 * n], F32, name="xw%d" % g)
+                xw[g] = w
+            nc.gpsimd.tensor_scalar(
+                out=xw[g][:, t * n : (t + 1) * n],
+                in0=xb[:, lo : lo + n],
+                scalar1=natural(0, t),
+                scalar2=natural(4, t),
+                op0=ALU.mult,
+                op1=ALU.add,
+            )
 
         def copy_z(j):
-            c = p2.tile([P, 2048], F32, name="zc", tag="zc")
+            c = p1.tile([P, 2048], F32, name="zc", tag="zc")
             n = SIZES[j]
             for t in range(4):
                 nc.scalar.copy(out=c[:, t * n : (t + 1) * n], in_=banks["z", j][t][:, 0:n])
@@ -260,11 +265,13 @@ def tile_grucell_t_kernel(
             for s in range(SIZES[j] // P):
                 bank = flp.tile([P, 512], F32, name="fl", tag="fl")
                 for t in range(4):
-                    lo = t * SIZES[j] + s * P
-                    for k, src in enumerate((zc[j], xw[j])):
+                    zlo = t * SIZES[j] + s * P
+                    g = (j + 1) // 2
+                    xlo = t * XG_SIZE[g] + STARTS[j] - XG_START[g] + s * P
+                    for k, src in enumerate((zc[j][:, zlo : zlo + P], xw[g][:, xlo : xlo + P])):
                         nc.tensor.matmul(
                             out=bank[:, t * P : (t + 1) * P],
-                            lhsT=src[:, lo : lo + P],
+                            lhsT=src,
                             rhs=ident[:],
                             is_transpose=True,
                             start=(k == 0),
@@ -274,7 +281,7 @@ def tile_grucell_t_kernel(
             zbank[j] = got
 
         def act_z(j):
-            u = p2.tile([P, 2048], F32, name="uu", tag="uu")
+            u = p1.tile([P, 2048], F32, name="uu", tag="uu")
             for s in range(SIZES[j] // P):
                 nc.scalar.activation(
                     out=u[:, s * D : (s + 1) * D], in_=zbank[j][s][:], func=ACT.Sigmoid, bias=0.0, scale=-1.0
@@ -310,9 +317,10 @@ def tile_grucell_t_kernel(
             for s in range(first, end):
                 cols = slice(s * D, (s + 1) * D)
                 nc.vector.tensor_tensor(out=o[:, cols], in0=uu[j][:, cols], in1=dbank[j][s][:], op=ALU.mult)
-                adder.tensor_tensor(out=o[:, cols], in0=o[:, cols], in1=hn[j][:, cols], op=ALU.add)
                 if (s + 1) % per == 0:
                     lo = s + 1 - per
+                    both = slice(lo * D, (s + 1) * D)
+                    adder.tensor_tensor(out=o[:, both], in0=o[:, both], in1=hn[j][:, both], op=ALU.add)
                     nc.sync.dma_start(
                         out=rows[:, lo : s + 1, :],
                         in_=o[:, lo * D : (s + 1) * D].rearrange("p (s c) -> p s c", s=per),
@@ -350,7 +358,10 @@ def tile_grucell_t_kernel(
         prep_params()
         prep_w_tr(Z_PLANE, "ss")
         banks["r", 0] = mx(R_PLANE, hcod[0], SIZES[0])
-        x_term(0)
+        x_list = [(g, t) for g in range(len(X_GROUPS)) for t in range(4)]
+        for g, t in x_list[:4]:
+            x_term(g, t)
+        x_done = 4
 
         for i in range(NBLK):
             gates_r(i)
@@ -382,8 +393,9 @@ def tile_grucell_t_kernel(
             if i > 0:
                 nsub = SIZES[i - 1] // P
                 blend(i - 1, nc.gpsimd, 2, 0, nsub if i < LAST else nsub // 2)
-            if i + 1 < NBLK:
-                x_term(i + 1)
+            for g, t in x_list[x_done : x_done + X_PLAN.get(i, 0)]:
+                x_term(g, t)
+            x_done = x_done + X_PLAN.get(i, 0)
 
         banks["g", LAST] = mx(G_PLANE, hrcod[LAST], SIZES[LAST])
         flip_z(LAST)

@@ -281,20 +281,25 @@ def tile_grucell_t_kernel(
             zbank[j] = got
 
         def act_z(j):
-            u = p1.tile([P, 2048], F32, name="uu", tag="uu")
+            u = p2.tile([P, 2048], F32, name="uu", tag="uu")
             for s in range(SIZES[j] // P):
                 nc.scalar.activation(
                     out=u[:, s * D : (s + 1) * D], in_=zbank[j][s][:], func=ACT.Sigmoid, bias=0.0, scale=-1.0
                 )
             uu[j] = u
 
+        def minus_h(bank, j, s, first):
+            nc.tensor.matmul(
+                out=bank[:], lhsT=negi[:], rhs=hn[j][:, s * D : (s + 1) * D], start=first, stop=not first
+            )
+
         def flip_t(j):
             got = []
             for s in range(SIZES[j] // P):
                 bank = flp.tile([P, 512], F32, name="fl", tag="fl")
-                nc.tensor.matmul(
-                    out=bank[:], lhsT=negi[:], rhs=hn[j][:, s * D : (s + 1) * D], start=True, stop=False
-                )
+                h_first = s % 2 == 0
+                if h_first:
+                    minus_h(bank, j, s, True)
                 for t in range(4):
                     lo = t * SIZES[j] + s * P
                     nc.tensor.matmul(
@@ -302,15 +307,17 @@ def tile_grucell_t_kernel(
                         lhsT=tt[j][:, lo : lo + P],
                         rhs=ident[:],
                         is_transpose=True,
-                        start=False,
-                        stop=(t == 3),
+                        start=(t == 0 and not h_first),
+                        stop=(t == 3 and h_first),
                     )
+                if not h_first:
+                    minus_h(bank, j, s, False)
                 got.append(bank)
             dbank[j] = got
 
         def blend(j, adder, per, first, end):
             if first == 0:
-                o = p3.tile([P, 2048], F32, name="ot", tag="ot")
+                o = p2.tile([P, 2048], F32, name="ot", tag="ot")
                 ot[j] = o
             o = ot[j]
             rows = out[STARTS[j] : STARTS[j] + SIZES[j], :].rearrange("(s p) c -> p s c", p=P)
@@ -328,7 +335,7 @@ def tile_grucell_t_kernel(
 
         def blend_last(j):
             nsub = SIZES[j] // P
-            o = p3.tile([P, 2048], F32, name="ot", tag="ot")
+            o = p2.tile([P, 2048], F32, name="ot", tag="ot")
             rows = out[STARTS[j] : STARTS[j] + SIZES[j], :].rearrange("(s p) c -> p s c", p=P)
             for s in range(nsub):
                 cols = slice(s * D, (s + 1) * D)

from contextlib import ExitStack

import concourse.mybir as mybir
from concourse.masks import make_identity

F32 = mybir.dt.float32
BF16 = mybir.dt.bfloat16
U32 = mybir.dt.uint32
U8 = mybir.dt.uint8
FP8X4 = mybir.dt.float8_e4m3fn_x4
ALU = mybir.AluOpType
ACT = mybir.ActivationFunctionType

P = 128
B = 4096
D = 512
SIZES = [256, 512, 512, 512, 512, 512, 512, 512, 256]
NBLK = len(SIZES)
STARTS = [sum(SIZES[:j]) for j in range(NBLK)]
LAST = NBLK - 1
FLOPS = 2 * B * D * 3 * D

R_PLANE = 0
Z_PLANE = 1
G_PLANE = 2
X_FIRST = SIZES[0]
X_GROUPS = [[0], [1, 2], [3, 4], [5, 6], [7, 8]]
XG_START = [STARTS[g[0]] for g in X_GROUPS]
XG_SIZE = [sum([SIZES[j] for j in g]) for g in X_GROUPS]
X_PLAN = {0: 5, 1: 2, 2: 2, 3: 2, 4: 2, 5: 2, 6: 1}
assert sum(SIZES) == B


def tile_grucell_t_kernel(
    tc, inputs, hidden, gate_w_I2H, gate_w_H2H, gate_bias, update_w_I2H, update_w_H2H, update_bias, out
):
    nc = tc.nc
    with ExitStack() as ctx:
        const = ctx.enter_context(tc.tile_pool(name="const", bufs=1))
        hpool = ctx.enter_context(tc.tile_pool(name="hpool", bufs=NBLK))
        p1 = ctx.enter_context(tc.tile_pool(name="p1", bufs=1))
        p2 = ctx.enter_context(tc.tile_pool(name="p2", bufs=2))
        p3 = ctx.enter_context(tc.tile_pool(name="p3", bufs=3))
        mxp = ctx.enter_context(tc.psum_pool(name="mxp", bufs=4))
        flp = ctx.enter_context(tc.psum_pool(name="flp", bufs=4))
        ctx.enter_context(tc.manual_schedule())

        ident = const.tile([P, P], F32, name="ident")
        make_identity(nc, ident[:])
        prn = const.tile([P, 256], BF16, name="prn")
        nc.vector.memset(prn[:], 0.0)
        warm = const.tile([P, 1], F32, name="warm")
        nc.vector.memset(warm[:], 0.0)

        wn = {}
        hn = {}

        def load_w(plane, rows):
            wnat = const.tile([P, 2048], BF16, name="wn%d" % plane)
            if plane == R_PLANE:
                for u in range(2):
                    nc.sync.dma_start(
                        out=wnat[:, u * 1024 : (u + 1) * 1024],
                        in_=rows[:, :, u * 256 : (u + 1) * 256, :].rearrange("a b (m e) k -> m (a b e k)", e=2),
                    )
            else:
                nc.sync.dma_start(
                    out=wnat[:].rearrange("m (t k) -> m t k", t=4),
                    in_=rows.rearrange("a b (t m) k -> m (a b t) k", t=4),
                )
            wn[plane] = wnat

        def load_h(queue, j):
            hnat = hpool.tile([P, 2048], BF16, name="hn", tag="hn")
            queue.dma_start(
                out=hnat[:, 0 : 4 * SIZES[j]].rearrange("p (s j) -> p s j", j=D),
                in_=hidden[STARTS[j] : STARTS[j] + SIZES[j], :].rearrange("(s p) j -> p s j", p=P),
            )
            hn[j] = hnat

        xb = const.tile([P, B], BF16, name="xb")
        xrow = inputs.rearrange("b o -> (b o)")
        nc.scalar.dma_start(out=prn[0:4, :], in_=gate_w_I2H.rearrange("a b (r k) c -> (a b r) (k c)", k=256))
        nc.scalar.dma_start(out=prn[4:8, :], in_=gate_bias.rearrange("(r k) -> r k", k=256))
        nc.scalar.dma_start(out=prn[8:10, :], in_=update_w_I2H.rearrange("a b (r k) c -> (a b r) (k c)", k=256))
        nc.scalar.dma_start(out=prn[10:12, :], in_=update_bias.rearrange("(r k) -> r k", k=256))
        nc.scalar.activation(out=warm[:], in_=warm[:], func=ACT.Sigmoid)
        load_w(R_PLANE, gate_w_H2H[:, :, D : 2 * D, :])
        load_h(nc.sync, 0)
        nc.sync.dma_start(out=xb[:, 0:X_FIRST], in_=xrow[0:X_FIRST].partition_broadcast(P))
        load_w(Z_PLANE, gate_w_H2H[:, :, 0:D, :])
        load_h(nc.sync, 1)
        load_w(G_PLANE, update_w_H2H)
        nc.sync.dma_start(out=xb[:, X_FIRST:B], in_=xrow[X_FIRST:B].partition_broadcast(P))
        for j in range(2, NBLK):
            load_h(nc.sync, j)

        negi = const.tile([P, P], BF16, name="negi")
        nc.gpsimd.tensor_scalar(out=negi[:], in0=ident[:], scalar1=-1.0, scalar2=0.0, op0=ALU.mult, op1=ALU.add)

        wc = const.tile([P, 3 * 512], U32, name="wc", align_bytes=64)
        ws = const.tile([P, 3 * 512], U8, name="ws", align_bytes=64)
        gws = {}

        def prep_w_tr(plane, engines):
            words = wn[plane][:].bitcast(F32)
            gw = const.tile([P, 2048], BF16, name="gw%d" % plane, align_bytes=64)
            gww = gw[:].bitcast(F32)
            for u in range(2):
                bank = flp.tile([P, 512], F32, name="fl", tag="fl")
                for e in range(2):
                    for kh in range(2):
                        nc.tensor.transpose(
                            out=bank[:, e * 256 + kh * 128 : e * 256 + kh * 128 + 128],
                            in_=words[:, (2 * u + e) * 256 + kh * 128 : (2 * u + e) * 256 + kh * 128 + 128],
                            identity=ident[:],
                        )
                dst = gww[:, u * 512 : (u + 1) * 512].rearrange("p (e m k) -> p e m k", e=2, k=2)
                src = bank[:].rearrange("p (e k m) -> p e m k", e=2, k=2)
                if engines[u] == "v":
                    nc.vector.tensor_copy(out=dst, in_=src)
                else:
                    nc.scalar.copy(out=dst, in_=src)
            gws[plane] = gw

        def prep_w_q(plane):
            nc.vector.quantize_mx(
                out=wc[:, plane * 512 : (plane + 1) * 512].bitcast(FP8X4),
                scales=ws[:, plane * 512 : (plane + 1) * 512],
                in_=gws[plane][:],
            )

        prnf = const.tile([P, 256], F32, name="prnf")
        prm = const.tile([P, 64], F32, name="prm")

        def prep_params_in():
            nc.vector.tensor_copy(out=prnf[:], in_=prn[:])

        def prep_params():
            bank = flp.tile([P, 512], F32, name="fl", tag="fl")
            views = [prnf[:, 0:128], prnf[:, 128:256], prnf[:, 0:256:2], prnf[:, 1:256:2]]
            for j in range(4):
                nc.tensor.transpose(out=bank[:, j * 128 : (j + 1) * 128], in_=views[j], identity=ident[:])
            nc.vector.tensor_copy(
                out=prm[:].rearrange("p (j r) -> p j r", j=4),
                in_=bank[:].rearrange("p (j r) -> p j r", j=4)[:, :, 0:16],
            )

        def paired(row, t):
            col = (2 + t % 2) * 16 + row + t // 2
            return prm[:, col : col + 1]

        def natural(row, t):
            col = (t % 2) * 16 + row + t // 2
            return prm[:, col : col + 1]

        gh = {}
        hbank = {}
        hcod = {}
        banks = {}
        rr = {}
        zc = {}
        xw = {}
        zbank = {}
        uu = {}
        tt = {}
        dbank = {}
        ot = {}
        ghr = {}
        hrcod = {}

        def tr_h(j):
            words = hn[j][:].bitcast(F32)
            got = []
            for first in range(0, SIZES[j] // P, 2):
                bank = flp.tile([P, 512], F32, name="fl", tag="fl")
                for sl in range(2):
                    for u in range(2):
                        nc.tensor.transpose(
                            out=bank[:, (u * 2 + sl) * 128 : (u * 2 + sl) * 128 + 128],
                            in_=words[:, (first + sl) * 256 + u * 128 : (first + sl) * 256 + u * 128 + 128],
                            identity=ident[:],
                        )
                got.append(bank)
            hbank[j] = got

        def ev_h(j):
            g = p3.tile([P, 2048], BF16, name="gh", tag="gh", align_bytes=64)
            gwords = g[:].bitcast(F32)
            for k, bank in enumerate(hbank[j]):
                nc.scalar.copy(
                    out=gwords[:, k * 512 : (k + 1) * 512].rearrange("p (n u) -> p n u", u=2),
                    in_=bank[:].rearrange("p (u n) -> p n u", u=2),
                )
            gh[j] = g

        def quantise(src, n, tagname):
            c = p2.tile([P, 512], U32, name=tagname + "c", tag=tagname + "c", align_bytes=64)
            s = p2.tile([P, 512], U8, name=tagname + "s", tag=tagname + "s", align_bytes=64)
            nc.vector.quantize_mx(out=c[:, 0:n].bitcast(FP8X4), scales=s[:, 0:n], in_=src[:, 0 : 4 * n])
            return (c, s)

        def mx(plane, cs, n):
            got = []
            for t in range(4):
                bank = mxp.tile([P, 512], F32, name="mx", tag="mx")
                col = plane * 512 + t * 128
                nc.tensor.matmul_mx(
                    out=bank[:, 0:n],
                    lhsT=wc[:, col : col + 128].bitcast(FP8X4),
                    lhsT_scale=ws[:, col : col + 128],
                    rhs=cs[0][:, 0:n].bitcast(FP8X4),
                    rhs_scale=cs[1][:, 0:n],
                    start=True,
                    stop=True,
                )
                got.append(bank)
            return got

        def xrow_of(j):
            return xb[:, STARTS[j] : STARTS[j] + SIZES[j]]

        def gate(j, src, dst, func, wcol, bcol):
            n = SIZES[j]
            for t in range(4):
                seg = dst[:, t * n : (t + 1) * n]
                nc.vector.scalar_tensor_tensor(
                    out=seg, in0=xrow_of(j), scalar=wcol(t), in1=src[t][:, 0:n], op0=ALU.mult, op1=ALU.add
                )
                nc.scalar.activation(out=seg, in_=seg, func=func, bias=bcol(t), scale=1.0)

        def gates_r(i):
            rtile = p1.tile([P, 2048], F32, name="rr", tag="rr")
            rr[i] = rtile
            gate(i, banks["r", i], rtile, ACT.Sigmoid, lambda t: paired(2, t), lambda t: paired(6, t))

        def gates_g(j):
            ttile = p1.tile([P, 2048], F32, name="tt", tag="tt")
            tt[j] = ttile
            gate(j, banks["g", j], ttile, ACT.Tanh, lambda t: natural(8, t), lambda t: natural(10, t))

        def x_term(g, t):
            lo, n = XG_START[g], XG_SIZE[g]
            if t == 0:
                w = const.tile([P, 4 * n], F32, name="xw%d" % g)
                xw[g] = w
            nc.gpsimd.tensor_scalar(
                out=xw[g][:, t * n : (t + 1) * n],
                in0=xb[:, lo : lo + n],
                scalar1=natural(0, t),
                scalar2=natural(4, t),
                op0=ALU.mult,
                op1=ALU.add,
            )

        def copy_z(j):
            c = p1.tile([P, 2048], F32, name="zc", tag="zc")
            n = SIZES[j]
            for t in range(4):
                nc.scalar.copy(out=c[:, t * n : (t + 1) * n], in_=banks["z", j][t][:, 0:n])
            zc[j] = c

        def flip_z(j):
            got = []
            for s in range(SIZES[j] // P):
                bank = flp.tile([P, 512], F32, name="fl", tag="fl")
                for t in range(4):
                    zlo = t * SIZES[j] + s * P
                    g = (j + 1) // 2
                    xlo = t * XG_SIZE[g] + STARTS[j] - XG_START[g] + s * P
                    for k, src in enumerate((zc[j][:, zlo : zlo + P], xw[g][:, xlo : xlo + P])):
                        nc.tensor.matmul(
                            out=bank[:, t * P : (t + 1) * P],
                            lhsT=src,
                            rhs=ident[:],
                            is_transpose=True,
                            start=(k == 0),
                            stop=(k == 1),
                        )
                got.append(bank)
            zbank[j] = got

        def act_z(j):
            u = p2.tile([P, 2048], F32, name="uu", tag="uu")
            for s in range(SIZES[j] // P):
                nc.scalar.activation(
                    out=u[:, s * D : (s + 1) * D], in_=zbank[j][s][:], func=ACT.Sigmoid, bias=0.0, scale=-1.0
                )
            uu[j] = u

        def minus_h(bank, j, s, first):
            nc.tensor.matmul(
                out=bank[:], lhsT=negi[:], rhs=hn[j][:, s * D : (s + 1) * D], start=first, stop=not first
            )

        def flip_t(j):
            got = []
            for s in range(SIZES[j] // P):
                bank = flp.tile([P, 512], F32, name="fl", tag="fl")
                h_first = s % 2 == 0
                if h_first:
                    minus_h(bank, j, s, True)
                for t in range(4):
                    lo = t * SIZES[j] + s * P
                    nc.tensor.matmul(
                        out=bank[:, t * P : (t + 1) * P],
                        lhsT=tt[j][:, lo : lo + P],
                        rhs=ident[:],
                        is_transpose=True,
                        start=(t == 0 and not h_first),
                        stop=(t == 3 and h_first),
                    )
                if not h_first:
                    minus_h(bank, j, s, False)
                got.append(bank)
            dbank[j] = got

        def blend(j, adder, per, first, end):
            if first == 0:
                o = p2.tile([P, 2048], F32, name="ot", tag="ot")
                ot[j] = o
            o = ot[j]
            rows = out[STARTS[j] : STARTS[j] + SIZES[j], :].rearrange("(s p) c -> p s c", p=P)
            for s in range(first, end):
                cols = slice(s * D, (s + 1) * D)
                nc.vector.tensor_tensor(out=o[:, cols], in0=uu[j][:, cols], in1=dbank[j][s][:], op=ALU.mult)
                if (s + 1) % per == 0:
                    lo = s + 1 - per
                    both = slice(lo * D, (s + 1) * D)
                    adder.tensor_tensor(out=o[:, both], in0=o[:, both], in1=hn[j][:, both], op=ALU.add)
                    nc.sync.dma_start(
                        out=rows[:, lo : s + 1, :],
                        in_=o[:, lo * D : (s + 1) * D].rearrange("p (s c) -> p s c", s=per),
                    )

        def blend_last(j):
            nsub = SIZES[j] // P
            o = p2.tile([P, 2048], F32, name="ot", tag="ot")
            rows = out[STARTS[j] : STARTS[j] + SIZES[j], :].rearrange("(s p) c -> p s c", p=P)
            for s in range(nsub):
                cols = slice(s * D, (s + 1) * D)
                nc.vector.tensor_tensor(out=o[:, cols], in0=uu[j][:, cols], in1=dbank[j][s][:], op=ALU.mult)
            for s in range(nsub):
                cols = slice(s * D, (s + 1) * D)
                nc.vector.tensor_tensor(out=o[:, cols], in0=o[:, cols], in1=hn[j][:, cols], op=ALU.add)
                nc.sync.dma_start(out=rows[:, s, :], in_=o[:, cols])

        def h_times_r(i):
            hrt = p2.tile([P, 2048], BF16, name="ghr", tag="ghr", align_bytes=64)
            ghr[i] = hrt
            words = slice(0, 4 * SIZES[i])
            nc.vector.tensor_tensor(
                out=hrt[:, words].rearrange("p (c i t) -> p c t i", i=4, t=4),
                in0=rr[i][:, words].rearrange("p (t c i) -> p c t i", t=4, i=4),
                in1=gh[i][:, words].rearrange("p (c i t) -> p c t i", i=4, t=4),
                op=ALU.mult,
            )

        prep_w_tr(R_PLANE, "vs")
        prep_params_in()
        tr_h(0)
        ev_h(0)
        prep_w_q(R_PLANE)
        hcod[0] = quantise(gh[0], SIZES[0], "h")
        prep_params()
        prep_w_tr(Z_PLANE, "ss")
        banks["r", 0] = mx(R_PLANE, hcod[0], SIZES[0])
        x_list = [(g, t) for g in range(len(X_GROUPS)) for t in range(4)]
        for g, t in x_list[:4]:
            x_term(g, t)
        x_done = 4

        for i in range(NBLK):
            gates_r(i)
            if i == 0:
                prep_w_q(Z_PLANE)
            if i + 1 < NBLK:
                tr_h(i + 1)
                ev_h(i + 1)
            if i > 0:
                banks["g", i - 1] = mx(G_PLANE, hrcod[i - 1], SIZES[i - 1])
                flip_z(i - 1)
                gates_g(i - 1)
            else:
                prep_w_tr(G_PLANE, "ss")
            banks["z", i] = mx(Z_PLANE, hcod[i], SIZES[i])
            if i > 0:
                act_z(i - 1)
            h_times_r(i)
            if i + 1 < NBLK:
                hcod[i + 1] = quantise(gh[i + 1], SIZES[i + 1], "h")
            hrcod[i] = quantise(ghr[i], SIZES[i], "r")
            if i == 0:
                prep_w_q(G_PLANE)
            if i > 0:
                flip_t(i - 1)
            copy_z(i)
            if i + 1 < NBLK:
                banks["r", i + 1] = mx(R_PLANE, hcod[i + 1], SIZES[i + 1])
            if i > 0:
                nsub = SIZES[i - 1] // P
                blend(i - 1, nc.gpsimd, 2, 0, nsub if i < LAST else nsub // 2)
            for g, t in x_list[x_done : x_done + X_PLAN.get(i, 0)]:
                x_term(g, t)
            x_done = x_done + X_PLAN.get(i, 0)

        banks["g", LAST] = mx(G_PLANE, hrcod[LAST], SIZES[LAST])
        flip_z(LAST)
        gates_g(LAST)
        blend(LAST - 1, nc.gpsimd, 1, SIZES[LAST - 1] // P // 2, SIZES[LAST - 1] // P)
        act_z(LAST)
        flip_t(LAST)
        blend_last(LAST)
